import numpy as np
import ml_dtypes


def mxq(x, axis, fmt="e4m3"):
    dtype, down = {"e4m3": (ml_dtypes.float8_e4m3fn, 7), "e5m2": (ml_dtypes.float8_e5m2, 14)}[fmt]
    v = np.moveaxis(np.asarray(x, np.float32).astype(ml_dtypes.bfloat16).astype(np.float64), axis, -1)
    blocks = v.reshape(v.shape[:-1] + (-1, 32))
    amax = np.abs(blocks).max(-1, keepdims=True)
    byte = np.maximum(np.where(amax > 0, np.frexp(amax)[1] - 1 + 127, 0) - down, 1)
    scale = np.exp2(byte - 127.0)
    codes = (blocks / scale).astype(np.float32).astype(dtype).astype(np.float64)
    return np.moveaxis((codes * scale).reshape(v.shape), -1, axis)


WIDE = False


def mx_kscale(k):
    if not WIDE:
        return np.ones(k)
    levels = np.array([10, -10, 5, -5, 0])
    if k % 512:
        return np.exp2(np.random.permutation(np.resize(levels, k // 32))).repeat(32)
    a = np.empty((k // 512, 16))
    for p in range(k // 512):
        a[p, :8] = np.random.permutation(np.resize(levels, 8))
        for g in range(8):
            far = levels[np.abs(levels - a[p, g]) >= 10]
            a[p, g + 8] = far[np.random.randint(len(far))]
    return np.exp2(a.ravel()).repeat(32)


BF16 = ml_dtypes.bfloat16


def bf(x):
    return np.asarray(x, np.float32).astype(BF16)


def f64(x):
    return np.asarray(x).astype(np.float64)


I, B, D, H, F = 512, 2, 1024, 8, 128
EPS = 1e-5


def setup_inputs():
    s = mx_kscale(D)
    return {"x": bf(np.random.standard_normal((I, B, D))),
            "gamma": bf((1.0 + 0.1 * np.random.standard_normal(D)) * s),
            "beta": bf(0.1 * np.random.standard_normal(D) * s),
            "Wq": bf(np.random.standard_normal((D, H * F)) * 1.5 / np.sqrt(D) / s[:, None]),
            "Wv": bf(np.random.standard_normal((D, H * F)) * 1.5 / np.sqrt(D) / s[:, None]),
            "u_bias": bf(np.random.standard_normal((H, F)) * 0.5),
            "v_bias": bf(np.random.standard_normal((H, F)) * 0.5)}


def reference(x, gamma, beta, Wq, Wv, u_bias, v_bias):
    x = f64(x)
    mu = x.mean(-1, keepdims=True)
    var = ((x - mu) ** 2).mean(-1, keepdims=True)
    h = (x - mu) / np.sqrt(var + EPS) * f64(gamma) + f64(beta)
    hq = mxq(h, 2, "e4m3")
    q = (hq @ mxq(f64(Wq), 0, "e4m3")).reshape(I, B, H, F)
    v = (hq @ mxq(f64(Wv), 0, "e4m3")).reshape(I, B, H, F)
    return q + f64(u_bias), q + f64(v_bias), q, v

@@ -1,0 +1,346 @@
+from contextlib import ExitStack
+
+import concourse.mybir as mybir
+from concourse.masks import make_identity
+
+F32 = mybir.dt.float32
+BF16 = mybir.dt.bfloat16
+U32 = mybir.dt.uint32
+U8 = mybir.dt.uint8
+I32 = mybir.dt.int32
+FP8X4 = mybir.dt.float8_e4m3fn_x4
+ACT = mybir.ActivationFunctionType
+ALU = mybir.AluOpType
+
+P = 128
+PACK = 4
+K_PASS = P * PACK
+TOKENS = 1024
+D_MODEL = 1024
+FEATURES = 1024
+PASSES = D_MODEL // K_PASS
+CHUNKS = D_MODEL // P
+TOKEN_TILES = TOKENS // P
+GROUP = 2
+GROUPS = TOKEN_TILES // GROUP
+GROUP_TOKENS = GROUP * P
+N_TILE = 512
+HALVES = FEATURES // N_TILE
+HEADS = 8
+W_PIECE = 256
+BN_WIDTH = 512
+EPS = 1e-5
+
+FLOPS = 2 * TOKENS * D_MODEL * 2 * FEATURES
+
+
+def regroup_views(grouped, planes):
+    dst = grouped.rearrange("p (c i) t -> p c t i", i=4)
+    src = planes.rearrange("p t (c i) -> p c t i", i=4)
+    return dst, src
+
+
+def tile_multiheadattentiowithrpe_pa_kernel(
+    tc, x, gamma, beta, Wq, Wv, u_bias, v_bias, out_0, out_1, out_2, out_3
+):
+    nc = tc.nc
+
+    x_view = x.rearrange("i b d -> (i b) d").rearrange("(p j) d -> p j d", j=TOKEN_TILES)
+    out_views = [
+        o.rearrange("i b h f -> (i b) (h f)").rearrange("(p j) n -> p j n", j=TOKEN_TILES)
+        for o in (out_0, out_1, out_2, out_3)
+    ]
+    w_views = [w.rearrange("(g p t) n -> g p t n", t=PACK, p=P) for w in (Wq, Wv)]
+
+    with ExitStack() as ctx:
+        const = ctx.enter_context(tc.tile_pool(name="const", bufs=1))
+        keep = ctx.enter_context(tc.tile_pool(name="keep", bufs=1))
+        small = ctx.enter_context(tc.tile_pool(name="small", bufs=4))
+        work = ctx.enter_context(tc.tile_pool(name="work", bufs=2))
+        stage = ctx.enter_context(tc.tile_pool(name="stage", bufs=3))
+        psum_t = ctx.enter_context(tc.psum_pool(name="psum_t", bufs=3))
+        psum_o = ctx.enter_context(tc.psum_pool(name="psum_o", bufs=5))
+        ctx.enter_context(tc.manual_schedule())
+
+        ident = const.tile([P, P], F32, name="ident")
+        make_identity(nc, ident[:])
+        ident_bf = const.tile([P, P], BF16, name="ident_bf")
+        make_identity(nc, ident_bf[:])
+
+        rows = const.tile([P, P], BF16, name="rows")
+        nc.vector.memset(rows[:], 0.0)
+        gb_rows = const.tile([P, K_PASS], BF16, name="gb_rows")
+        nc.vector.memset(gb_rows[:], 0.0)
+        eps = const.tile([P, 1], F32, name="eps")
+        nc.vector.memset(eps[:], EPS)
+        warm = const.tile([P, 1], F32, name="warm")
+        nc.scalar.activation(out=warm[:], in_=eps[:], func=ACT.Sqrt)
+
+        x_sb = [keep.tile([P, GROUP, D_MODEL], BF16, name="x_sb%d" % grp) for grp in range(GROUPS)]
+        w_raw = [
+            [keep.tile([P, PACK, FEATURES], BF16, name="w_raw%d%d" % (w, g)) for g in range(PASSES)]
+            for w in range(2)
+        ]
+
+        def load_x(grp):
+            nc.sync.dma_start(out=x_sb[grp][:], in_=x_view[:, grp * GROUP : (grp + 1) * GROUP, :])
+
+        def load_w(w):
+            for g in range(PASSES):
+                nc.sync.dma_start(out=w_raw[w][g][:], in_=w_views[w][g])
+
+        load_x(0)
+        for i, vec in enumerate((gamma, beta)):
+            nc.sync.dma_start(
+                out=gb_rows[i * PASSES : (i + 1) * PASSES, :], in_=vec.rearrange("(g m) -> g m", m=K_PASS)
+            )
+        for i, vec in enumerate((u_bias, v_bias)):
+            nc.sync.dma_start(out=rows[i * HEADS : (i + 1) * HEADS, :], in_=vec)
+        load_w(0)
+        load_x(1)
+        load_w(1)
+        load_x(2)
+        load_x(3)
+
+        gb_cols = const.tile([P, 2 * CHUNKS], F32, name="gb_cols")
+        uv_cols = const.tile([P, 2 * HEADS], BF16, name="uv_cols")
+
+        def rows_to_columns():
+            cols_ps = psum_t.tile([P, P], BF16, tag="xt")
+            nc.tensor.transpose(cols_ps[:], rows[:], ident_bf[:])
+            nc.vector.tensor_copy(out=uv_cols[:], in_=cols_ps[:, 0 : 2 * HEADS])
+            gb_ps = psum_t.tile([P, PACK, P], BF16, tag="xt")
+            for t in range(PACK):
+                nc.tensor.transpose(gb_ps[:, t, :], gb_rows[:, t : K_PASS : PACK], ident_bf[:])
+            nc.vector.tensor_copy(
+                out=gb_cols[:].rearrange("p (w t) -> p w t", t=PACK),
+                in_=gb_ps[:, :, 0 : 2 * PASSES].rearrange("p t w -> p w t"),
+            )
+
+        def spread_biases():
+            for b in range(2 * HALVES):
+                bias_ps = psum_o.tile([P, N_TILE], F32, tag="acc")
+                for i in range(N_TILE // P):
+                    c = b * (N_TILE // P) + i
+                    nc.tensor.matmul(
+                        bias_ps[:, i * P : (i + 1) * P],
+                        lhsT=uv_cols[:, c : c + 1].to_broadcast([P, P]),
+                        rhs=ident_bf[:],
+                        start=True,
+                        stop=True,
+                    )
+                nc.scalar.copy(
+                    out=bias_all[:].rearrange("p b n -> p (b n)")[:, b * N_TILE : (b + 1) * N_TILE],
+                    in_=bias_ps[:],
+                )
+
+        bias_all = const.tile([P, 2, FEATURES], F32, name="bias_all")
+
+        h_codes = keep.tile([P, GROUPS * PASSES * GROUP_TOKENS], U32, name="h_codes", align_bytes=64)
+        h_scales = keep.tile([P, GROUPS * PASSES * GROUP_TOKENS], U8, name="h_scales", align_bytes=64)
+        w_codes = keep.tile([P, 2 * HALVES * PASSES * N_TILE], U32, name="w_codes", align_bytes=64)
+        w_scales = keep.tile([P, 2 * HALVES * PASSES * N_TILE], U8, name="w_scales", align_bytes=64)
+
+        w_grouped = {}
+
+        def regroup_w(w, half, g, copy):
+            if g == 0:
+                w_grouped[(w, half)] = work.tile(
+                    [P, PASSES, N_TILE, PACK], BF16, name="w_grouped", tag="w_grouped", align_bytes=64
+                )
+            for c0 in range(0, N_TILE, W_PIECE):
+                dst, src = regroup_views(
+                    w_grouped[(w, half)][:, g, c0 : c0 + W_PIECE, :],
+                    w_raw[w][g][:, :, half * N_TILE + c0 : half * N_TILE + c0 + W_PIECE],
+                )
+                copy(out=dst, in_=src)
+
+        def quantise_w(w, half):
+            block = w * HALVES + half
+            cols = slice(block * PASSES * N_TILE, (block + 1) * PASSES * N_TILE)
+            nc.vector.quantize_mx(
+                out=w_codes[:, cols].bitcast(FP8X4),
+                scales=w_scales[:, cols],
+                in_=w_grouped[(w, half)][:].rearrange("p g n t -> p (g n t)"),
+            )
+
+        mean_var = {}
+        std = {}
+        rstd = {}
+        normed = {}
+        h_planes = {}
+
+        def token_statistics(grp):
+            mean_var[grp] = small.tile([P, GROUP, 2], F32, name="mean_var", tag="mean_var")
+            stats = small.tile([P, GROUP, D_MODEL // BN_WIDTH, 6], F32, tag="stats")
+            for jj in range(GROUP):
+                for s in range(D_MODEL // BN_WIDTH):
+                    nc.vector.bn_stats(
+                        out=stats[:, jj, s, :], in_=x_sb[grp][:, jj, s * BN_WIDTH : (s + 1) * BN_WIDTH]
+                    )
+            for jj in range(GROUP):
+                nc.vector.bn_aggr(
+                    out=mean_var[grp][:, jj, :], in_=stats[:, jj, :, :].rearrange("p s v -> p (s v)")
+                )
+
+        def standard_deviation(grp):
+            std[grp] = small.tile([P, GROUP], F32, name="std", tag="std")
+            nc.scalar.activation(
+                out=std[grp][:], in_=mean_var[grp][:, :, 1], func=ACT.Sqrt, bias=eps[:, 0:1]
+            )
+
+        def normalise(grp):
+            rstd[grp] = small.tile([P, GROUP], F32, name="rstd", tag="rstd")
+            nc.vector.reciprocal(out=rstd[grp][:], in_=std[grp][:])
+            normed[grp] = []
+            for jj in range(GROUP):
+                xn = work.tile([P, D_MODEL], F32, tag="xn", bufs=2 * GROUP)
+                nc.vector.tensor_scalar(
+                    out=xn[:].rearrange("q (g t p) -> q g t p", t=PACK, p=P),
+                    in0=x_sb[grp][:, jj, :].rearrange("q (g p t) -> q g t p", t=PACK, p=P),
+                    scalar1=mean_var[grp][:, jj, 0:1],
+                    scalar2=rstd[grp][:, jj : jj + 1],
+                    op0=ALU.subtract,
+                    op1=ALU.mult,
+                )
+                normed[grp].append(xn)
+
+        def transpose_and_scale(grp):
+            h_planes[grp] = work.tile([P, CHUNKS, GROUP_TOKENS], BF16, name="h_planes", tag="h_planes")
+            for pair in range(CHUNKS // 2):
+                xt = psum_t.tile([P, 2, GROUP_TOKENS], F32, tag="xt")
+                for cc in range(2):
+                    c = 2 * pair + cc
+                    for jj in range(GROUP):
+                        nc.tensor.transpose(
+                            xt[:, cc, jj * P : (jj + 1) * P], normed[grp][jj][:, c * P : (c + 1) * P], ident[:]
+                        )
+                for cc in range(2):
+                    c = 2 * pair + cc
+                    nc.scalar.activation(
+                        out=h_planes[grp][:, c, :],
+                        in_=xt[:, cc, :],
+                        func=ACT.Identity,
+                        scale=gb_cols[:, c : c + 1],
+                        bias=gb_cols[:, CHUNKS + c : CHUNKS + c + 1],
+                    )
+
+        h_grouped = {}
+
+        def regroup_h(grp):
+            h_grouped[grp] = work.tile(
+                [P, PASSES, GROUP_TOKENS, PACK], BF16, name="h_grouped", tag="h_grouped", align_bytes=64
+            )
+            for g in range(PASSES):
+                dst, src = regroup_views(
+                    h_grouped[grp][:, g, :, :], h_planes[grp][:, g * PACK : (g + 1) * PACK, :]
+                )
+                nc.vector.tensor_copy(out=dst, in_=src)
+
+        def quantise_h(grp):
+            cols = slice(grp * PASSES * GROUP_TOKENS, (grp + 1) * PASSES * GROUP_TOKENS)
+            nc.vector.quantize_mx(
+                out=h_codes[:, cols].bitcast(FP8X4),
+                scales=h_scales[:, cols],
+                in_=h_grouped[grp][:].rearrange("p g r t -> p (g r t)"),
+            )
+
+        def project(j, block):
+            grp, jj = divmod(j, GROUP)
+            acc = psum_o.tile([P, N_TILE], F32, tag="acc")
+            for g in range(PASSES):
+                h_cols = slice(
+                    (grp * PASSES + g) * GROUP_TOKENS + jj * P, (grp * PASSES + g) * GROUP_TOKENS + (jj + 1) * P
+                )
+                w_cols = slice((block * PASSES + g) * N_TILE, (block * PASSES + g + 1) * N_TILE)
+                nc.tensor.matmul_mx(
+                    out=acc[:],
+                    lhsT=h_codes[:, h_cols].bitcast(FP8X4),
+                    lhsT_scale=h_scales[:, h_cols],
+                    rhs=w_codes[:, w_cols].bitcast(FP8X4),
+                    rhs_scale=w_scales[:, w_cols],
+                    start=(g == 0),
+                    stop=(g == PASSES - 1),
+                )
+            return acc
+
+        def store_keys(j, banks):
+            keys = stage.tile([P, FEATURES], F32, tag="keys")
+            for half in range(HALVES):
+                nc.scalar.copy(out=keys[:, half * N_TILE : (half + 1) * N_TILE], in_=banks[half][:])
+            nc.sync.dma_start(out=out_views[2][:, j, :], in_=keys[:])
+
+        biased = {}
+
+        def add_biases(j, half, bank):
+            if half == 0:
+                biased[j] = stage.tile([P, 2, FEATURES], F32, name="biased", tag="biased")
+            cols = slice(half * N_TILE, (half + 1) * N_TILE)
+            nc.vector.tensor_tensor(
+                out=biased[j][:, :, cols],
+                in0=bank[:].unsqueeze(1).to_broadcast([P, 2, N_TILE]),
+                in1=bias_all[:, :, cols],
+                op=ALU.add,
+            )
+
+        def store_biased(j):
+            nc.sync.dma_start(out=out_views[0][:, j, :], in_=biased[j][:, 0, :])
+            nc.sync.dma_start(out=out_views[1][:, j, :], in_=biased[j][:, 1, :])
+
+        def values(j):
+            vals = stage.tile([P, FEATURES], F32, tag="vals")
+            for half in range(HALVES):
+                acc = project(j, HALVES + half)
+                nc.scalar.copy(out=vals[:, half * N_TILE : (half + 1) * N_TILE], in_=acc[:])
+            nc.sync.dma_start(out=out_views[3][:, j, :], in_=vals[:])
+
+        def scalar_spare_time(slot):
+            if slot < HALVES * PASSES:
+                regroup_w(1, slot // PASSES, slot % PASSES, nc.scalar.copy)
+            else:
+                for j in range(GROUP * (slot - HALVES * PASSES), GROUP * (slot - HALVES * PASSES + 1)):
+                    if j < TOKEN_TILES:
+                        values(j)
+
+        token_statistics(0)
+        standard_deviation(0)
+        rows_to_columns()
+        regroup_w(0, 0, 0, nc.vector.tensor_copy)
+        normalise(0)
+        regroup_w(0, 1, 0, nc.scalar.copy)
+        transpose_and_scale(0)
+        spread_biases()
+        regroup_w(0, 0, 1, nc.vector.tensor_copy)
+        regroup_w(0, 1, 1, nc.vector.tensor_copy)
+        quantise_w(0, 0)
+        regroup_h(0)
+        quantise_w(0, 1)
+        quantise_h(0)
+        scalar_spare_time(0)
+
+        for grp in range(GROUPS):
+            first, second = GROUP * grp, GROUP * grp + 1
+            more = grp + 1 < GROUPS
+            banks = {j: [project(j, half) for half in range(HALVES)] for j in (first, second)}
+            if more:
+                token_statistics(grp + 1)
+            store_keys(first, banks[first])
+            add_biases(first, 0, banks[first][0])
+            if more:
+                standard_deviation(grp + 1)
+                normalise(grp + 1)
+            store_keys(second, banks[second])
+            scalar_spare_time(2 * grp + 1)
+            add_biases(first, 1, banks[first][1])
+            store_biased(first)
+            add_biases(second, 0, banks[second][0])
+            add_biases(second, 1, banks[second][1])
+            store_biased(second)
+            if more:
+                transpose_and_scale(grp + 1)
+            if grp < HALVES:
+                quantise_w(1, grp)
+            scalar_spare_time(2 * grp + 2)
+            if more:
+                regroup_h(grp + 1)
+                quantise_h(grp + 1)

@@ -7,7 +7,6 @@ F32 = mybir.dt.float32
 BF16 = mybir.dt.bfloat16
 U32 = mybir.dt.uint32
 U8 = mybir.dt.uint8
-I32 = mybir.dt.int32
 FP8X4 = mybir.dt.float8_e4m3fn_x4
 ACT = mybir.ActivationFunctionType
 ALU = mybir.AluOpType
@@ -19,14 +18,11 @@ TOKENS = 1024
 D_MODEL = 1024
 FEATURES = 1024
 PASSES = D_MODEL // K_PASS
-CHUNKS = D_MODEL // P
+PLANES = PASSES * PACK
 TOKEN_TILES = TOKENS // P
-GROUP = 2
-GROUPS = TOKEN_TILES // GROUP
-GROUP_TOKENS = GROUP * P
+GROUPS = ((0,), (1,), (2, 3), (4, 5), (6, 7))
 N_TILE = 512
 HALVES = FEATURES // N_TILE
-HEADS = 8
 W_PIECE = 256
 BN_WIDTH = 512
 EPS = 1e-5
@@ -62,285 +58,375 @@ def tile_multiheadattentiowithrpe_pa_kernel(
         psum_o = ctx.enter_context(tc.psum_pool(name="psum_o", bufs=5))
         ctx.enter_context(tc.manual_schedule())
 
-        ident = const.tile([P, P], F32, name="ident")
-        make_identity(nc, ident[:])
         ident_bf = const.tile([P, P], BF16, name="ident_bf")
         make_identity(nc, ident_bf[:])
+        ident = const.tile([P, P], F32, name="ident")
+        make_identity(nc, ident[:])
 
-        rows = const.tile([P, P], BF16, name="rows")
+        rows = const.tile([P, FEATURES], BF16, name="rows")
         nc.vector.memset(rows[:], 0.0)
-        gb_rows = const.tile([P, K_PASS], BF16, name="gb_rows")
-        nc.vector.memset(gb_rows[:], 0.0)
         eps = const.tile([P, 1], F32, name="eps")
         nc.vector.memset(eps[:], EPS)
         warm = const.tile([P, 1], F32, name="warm")
-        nc.scalar.activation(out=warm[:], in_=eps[:], func=ACT.Sqrt)
+        nc.scalar.activation(out=warm[:], in_=eps[:], func=ACT.Abs_reciprocal_sqrt)
 
-        x_sb = [keep.tile([P, GROUP, D_MODEL], BF16, name="x_sb%d" % grp) for grp in range(GROUPS)]
+        x_sb = [
+            keep.tile([P, len(tiles), D_MODEL], BF16, name="x_sb%d" % grp) for grp, tiles in enumerate(GROUPS)
+        ]
         w_raw = [
-            [keep.tile([P, PACK, FEATURES], BF16, name="w_raw%d%d" % (w, g)) for g in range(PASSES)]
+            [
+                [keep.tile([P, PACK, N_TILE], BF16, name="w_raw%d%d%d" % (w, half, g)) for g in range(PASSES)]
+                for half in range(HALVES)
+            ]
             for w in range(2)
         ]
 
         def load_x(grp):
-            nc.sync.dma_start(out=x_sb[grp][:], in_=x_view[:, grp * GROUP : (grp + 1) * GROUP, :])
+            tiles = GROUPS[grp]
+            nc.sync.dma_start(out=x_sb[grp][:], in_=x_view[:, tiles[0] : tiles[-1] + 1, :])
 
-        def load_w(w):
+        def load_w(w, half):
             for g in range(PASSES):
-                nc.sync.dma_start(out=w_raw[w][g][:], in_=w_views[w][g])
+                nc.sync.dma_start(
+                    out=w_raw[w][half][g][:], in_=w_views[w][g][:, :, half * N_TILE : (half + 1) * N_TILE]
+                )
 
         load_x(0)
-        for i, vec in enumerate((gamma, beta)):
-            nc.sync.dma_start(
-                out=gb_rows[i * PASSES : (i + 1) * PASSES, :], in_=vec.rearrange("(g m) -> g m", m=K_PASS)
-            )
-        for i, vec in enumerate((u_bias, v_bias)):
-            nc.sync.dma_start(out=rows[i * HEADS : (i + 1) * HEADS, :], in_=vec)
-        load_w(0)
+        for i, vec in enumerate((u_bias.rearrange("h f -> (h f)"), v_bias.rearrange("h f -> (h f)"), gamma, beta)):
+            nc.sync.dma_start(out=rows[i : i + 1, :], in_=vec.unsqueeze(0))
         load_x(1)
-        load_w(1)
+        load_w(0, 0)
+        load_w(0, 1)
+        load_w(1, 0)
         load_x(2)
+        load_w(1, 1)
         load_x(3)
+        load_x(4)
 
-        gb_cols = const.tile([P, 2 * CHUNKS], F32, name="gb_cols")
-        uv_cols = const.tile([P, 2 * HEADS], BF16, name="uv_cols")
+        gb_cols = const.tile([P, 2 * PLANES], F32, name="gb_cols")
+        bias_all = const.tile([P, 2, FEATURES], F32, name="bias_all")
 
-        def rows_to_columns():
-            cols_ps = psum_t.tile([P, P], BF16, tag="xt")
-            nc.tensor.transpose(cols_ps[:], rows[:], ident_bf[:])
-            nc.vector.tensor_copy(out=uv_cols[:], in_=cols_ps[:, 0 : 2 * HEADS])
-            gb_ps = psum_t.tile([P, PACK, P], BF16, tag="xt")
-            for t in range(PACK):
-                nc.tensor.transpose(gb_ps[:, t, :], gb_rows[:, t : K_PASS : PACK], ident_bf[:])
-            nc.vector.tensor_copy(
-                out=gb_cols[:].rearrange("p (w t) -> p w t", t=PACK),
-                in_=gb_ps[:, :, 0 : 2 * PASSES].rearrange("p t w -> p w t"),
-            )
-
-        def spread_biases():
-            for b in range(2 * HALVES):
-                bias_ps = psum_o.tile([P, N_TILE], F32, tag="acc")
-                for i in range(N_TILE // P):
-                    c = b * (N_TILE // P) + i
+        def gamma_beta_columns():
+            cols_ps = psum_t.tile([P, PLANES, 2], F32, tag="xt")
+            for g in range(PASSES):
+                for t in range(PACK):
                     nc.tensor.matmul(
-                        bias_ps[:, i * P : (i + 1) * P],
-                        lhsT=uv_cols[:, c : c + 1].to_broadcast([P, P]),
-                        rhs=ident_bf[:],
+                        cols_ps[:, g * PACK + t, :],
+                        lhsT=rows[:, g * K_PASS + t : (g + 1) * K_PASS : PACK],
+                        rhs=ident_bf[:, 2:4],
                         start=True,
                         stop=True,
                     )
-                nc.scalar.copy(
-                    out=bias_all[:].rearrange("p b n -> p (b n)")[:, b * N_TILE : (b + 1) * N_TILE],
-                    in_=bias_ps[:],
-                )
+            nc.vector.tensor_copy(
+                out=gb_cols[:].rearrange("p (v c) -> p v c", c=PLANES), in_=cols_ps[:].rearrange("p c v -> p v c")
+            )
 
-        bias_all = const.tile([P, 2, FEATURES], F32, name="bias_all")
+        def spread_bias(b, half, copy):
+            bias_ps = psum_o.tile([P, N_TILE], F32, tag="acc")
+            nc.tensor.matmul(
+                bias_ps[:],
+                lhsT=ident_bf[:, b : b + 1].to_broadcast([P, P]),
+                rhs=rows[:, half * N_TILE : (half + 1) * N_TILE],
+                start=True,
+                stop=True,
+            )
+            copy(out=bias_all[:, b, half * N_TILE : (half + 1) * N_TILE], in_=bias_ps[:])
 
-        h_codes = keep.tile([P, GROUPS * PASSES * GROUP_TOKENS], U32, name="h_codes", align_bytes=64)
-        h_scales = keep.tile([P, GROUPS * PASSES * GROUP_TOKENS], U8, name="h_scales", align_bytes=64)
-        w_codes = keep.tile([P, 2 * HALVES * PASSES * N_TILE], U32, name="w_codes", align_bytes=64)
-        w_scales = keep.tile([P, 2 * HALVES * PASSES * N_TILE], U8, name="w_scales", align_bytes=64)
+        h_codes = [
+            keep.tile([P, PASSES * len(tiles) * P], U32, name="h_codes%d" % grp, align_bytes=64)
+            for grp, tiles in enumerate(GROUPS)
+        ]
+        h_scales = [
+            keep.tile([P, PASSES * len(tiles) * P], U8, name="h_scales%d" % grp, align_bytes=64)
+            for grp, tiles in enumerate(GROUPS)
+        ]
+        w_codes = [
+            [keep.tile([P, PASSES * N_TILE], U32, name="w_codes%d%d" % (w, h), align_bytes=64) for h in range(HALVES)]
+            for w in range(2)
+        ]
+        w_scales = [
+            [keep.tile([P, PASSES * N_TILE], U8, name="w_scales%d%d" % (w, h), align_bytes=64) for h in range(HALVES)]
+            for w in range(2)
+        ]
+        w_grouped = [
+            [
+                work.tile([P, PASSES, N_TILE, PACK], BF16, name="w_grouped%d%d" % (w, h), bufs=1, align_bytes=64)
+                for h in range(HALVES)
+            ]
+            for w in range(2)
+        ]
 
-        w_grouped = {}
+        def gpsimd_copy(out, in_):
+            nc.gpsimd.tensor_scalar(out=out, in0=in_, scalar1=1.0, scalar2=0.0, op0=ALU.mult, op1=ALU.add)
 
-        def regroup_w(w, half, g, copy):
-            if g == 0:
-                w_grouped[(w, half)] = work.tile(
-                    [P, PASSES, N_TILE, PACK], BF16, name="w_grouped", tag="w_grouped", align_bytes=64
-                )
-            for c0 in range(0, N_TILE, W_PIECE):
-                dst, src = regroup_views(
-                    w_grouped[(w, half)][:, g, c0 : c0 + W_PIECE, :],
-                    w_raw[w][g][:, :, half * N_TILE + c0 : half * N_TILE + c0 + W_PIECE],
-                )
-                copy(out=dst, in_=src)
+        def regroup_w(w, half, g, piece, copy):
+            cols = slice(piece * W_PIECE, (piece + 1) * W_PIECE)
+            dst, src = regroup_views(w_grouped[w][half][:, g, cols, :], w_raw[w][half][g][:, :, cols])
+            copy(out=dst, in_=src)
 
         def quantise_w(w, half):
-            block = w * HALVES + half
-            cols = slice(block * PASSES * N_TILE, (block + 1) * PASSES * N_TILE)
             nc.vector.quantize_mx(
-                out=w_codes[:, cols].bitcast(FP8X4),
-                scales=w_scales[:, cols],
-                in_=w_grouped[(w, half)][:].rearrange("p g n t -> p (g n t)"),
+                out=w_codes[w][half][:].bitcast(FP8X4),
+                scales=w_scales[w][half][:],
+                in_=w_grouped[w][half][:].rearrange("p g n t -> p (g n t)"),
             )
 
         mean_var = {}
-        std = {}
         rstd = {}
+        shift = {}
         normed = {}
         h_planes = {}
+        h_grouped = {}
 
-        def token_statistics(grp):
-            mean_var[grp] = small.tile([P, GROUP, 2], F32, name="mean_var", tag="mean_var")
-            stats = small.tile([P, GROUP, D_MODEL // BN_WIDTH, 6], F32, tag="stats")
-            for jj in range(GROUP):
-                for s in range(D_MODEL // BN_WIDTH):
-                    nc.vector.bn_stats(
-                        out=stats[:, jj, s, :], in_=x_sb[grp][:, jj, s * BN_WIDTH : (s + 1) * BN_WIDTH]
-                    )
-            for jj in range(GROUP):
-                nc.vector.bn_aggr(
-                    out=mean_var[grp][:, jj, :], in_=stats[:, jj, :, :].rearrange("p s v -> p (s v)")
+        def token_statistics(grp, jj):
+            n = len(GROUPS[grp])
+            if jj == 0:
+                mean_var[grp] = small.tile([P, n, 2], F32, name="mean_var", tag="mean_var")
+            stats = small.tile([P, D_MODEL // BN_WIDTH, 6], F32, name="stats", tag="stats")
+            for s in range(D_MODEL // BN_WIDTH):
+                nc.vector.bn_stats(
+                    out=stats[:, s, :], in_=x_sb[grp][:, jj, s * BN_WIDTH : (s + 1) * BN_WIDTH]
                 )
+            nc.vector.bn_aggr(out=mean_var[grp][:, jj, :], in_=stats[:].rearrange("p s v -> p (s v)"))
 
-        def standard_deviation(grp):
-            std[grp] = small.tile([P, GROUP], F32, name="std", tag="std")
+        def inverse_deviation(grp):
+            n = len(GROUPS[grp])
+            rstd[grp] = small.tile([P, n], F32, name="rstd", tag="rstd")
             nc.scalar.activation(
-                out=std[grp][:], in_=mean_var[grp][:, :, 1], func=ACT.Sqrt, bias=eps[:, 0:1]
+                out=rstd[grp][:], in_=mean_var[grp][:, :, 1], func=ACT.Abs_reciprocal_sqrt, bias=eps[:, 0:1]
             )
 
-        def normalise(grp):
-            rstd[grp] = small.tile([P, GROUP], F32, name="rstd", tag="rstd")
-            nc.vector.reciprocal(out=rstd[grp][:], in_=std[grp][:])
-            normed[grp] = []
-            for jj in range(GROUP):
-                xn = work.tile([P, D_MODEL], F32, tag="xn", bufs=2 * GROUP)
-                nc.vector.tensor_scalar(
-                    out=xn[:].rearrange("q (g t p) -> q g t p", t=PACK, p=P),
-                    in0=x_sb[grp][:, jj, :].rearrange("q (g p t) -> q g t p", t=PACK, p=P),
-                    scalar1=mean_var[grp][:, jj, 0:1],
-                    scalar2=rstd[grp][:, jj : jj + 1],
-                    op0=ALU.subtract,
-                    op1=ALU.mult,
-                )
-                normed[grp].append(xn)
+        def minus_mean(grp):
+            n = len(GROUPS[grp])
+            shift[grp] = small.tile([P, n], F32, name="shift", tag="shift")
+            nc.vector.scalar_tensor_tensor(
+                out=shift[grp][:], in0=mean_var[grp][:, :, 0], scalar=-1.0, in1=rstd[grp][:], op0=ALU.mult, op1=ALU.mult
+            )
 
-        def transpose_and_scale(grp):
-            h_planes[grp] = work.tile([P, CHUNKS, GROUP_TOKENS], BF16, name="h_planes", tag="h_planes")
-            for pair in range(CHUNKS // 2):
-                xt = psum_t.tile([P, 2, GROUP_TOKENS], F32, tag="xt")
-                for cc in range(2):
-                    c = 2 * pair + cc
-                    for jj in range(GROUP):
+        def normalise(grp, jj, engines):
+            if jj == 0:
+                normed[grp] = []
+            xn = work.tile([P, D_MODEL], F32, name="xn", tag="xn", bufs=4)
+            for g in range(PASSES):
+                cols = slice(g * K_PASS, (g + 1) * K_PASS)
+                dst = xn[:, cols].rearrange("q (t p) -> q t p", t=PACK)
+                src = x_sb[grp][:, jj, cols].rearrange("q (p t) -> q t p", t=PACK)
+                if engines[g] == "scalar":
+                    nc.scalar.activation(
+                        out=dst,
+                        in_=src,
+                        func=ACT.Identity,
+                        scale=rstd[grp][:, jj : jj + 1],
+                        bias=shift[grp][:, jj : jj + 1],
+                    )
+                else:
+                    (nc.gpsimd if engines[g] == "gpsimd" else nc.vector).tensor_scalar(
+                        out=dst,
+                        in0=src,
+                        scalar1=mean_var[grp][:, jj, 0:1],
+                        scalar2=rstd[grp][:, jj : jj + 1],
+                        op0=ALU.subtract,
+                        op1=ALU.mult,
+                    )
+            normed[grp].append(xn)
+
+        def transpose_and_scale(grp, g):
+            n = len(GROUPS[grp])
+            per_bank = PACK // n
+            if g == 0:
+                h_planes[grp] = work.tile([P, PLANES, n * P], BF16, name="h_planes", tag="h_planes%d" % n)
+            for c0 in range(g * PACK, (g + 1) * PACK, per_bank):
+                xt = psum_t.tile([P, per_bank, n * P], F32, name="xt", tag="xt")
+                for cc in range(per_bank):
+                    c = c0 + cc
+                    for jj in range(n):
                         nc.tensor.transpose(
                             xt[:, cc, jj * P : (jj + 1) * P], normed[grp][jj][:, c * P : (c + 1) * P], ident[:]
                         )
-                for cc in range(2):
-                    c = 2 * pair + cc
+                for cc in range(per_bank):
+                    c = c0 + cc
                     nc.scalar.activation(
                         out=h_planes[grp][:, c, :],
                         in_=xt[:, cc, :],
                         func=ACT.Identity,
                         scale=gb_cols[:, c : c + 1],
-                        bias=gb_cols[:, CHUNKS + c : CHUNKS + c + 1],
+                        bias=gb_cols[:, PLANES + c : PLANES + c + 1],
                     )
 
-        h_grouped = {}
-
-        def regroup_h(grp):
-            h_grouped[grp] = work.tile(
-                [P, PASSES, GROUP_TOKENS, PACK], BF16, name="h_grouped", tag="h_grouped", align_bytes=64
-            )
-            for g in range(PASSES):
-                dst, src = regroup_views(
-                    h_grouped[grp][:, g, :, :], h_planes[grp][:, g * PACK : (g + 1) * PACK, :]
+        def regroup_h(grp, g, copy):
+            n = len(GROUPS[grp])
+            if g == 0:
+                h_grouped[grp] = work.tile(
+                    [P, PASSES, n * P, PACK], BF16, name="h_grouped", tag="h_grouped%d" % n, align_bytes=64
                 )
-                nc.vector.tensor_copy(out=dst, in_=src)
+            dst, src = regroup_views(
+                h_grouped[grp][:, g, :, :], h_planes[grp][:, g * PACK : (g + 1) * PACK, :]
+            )
+            copy(out=dst, in_=src)
 
         def quantise_h(grp):
-            cols = slice(grp * PASSES * GROUP_TOKENS, (grp + 1) * PASSES * GROUP_TOKENS)
             nc.vector.quantize_mx(
-                out=h_codes[:, cols].bitcast(FP8X4),
-                scales=h_scales[:, cols],
+                out=h_codes[grp][:].bitcast(FP8X4),
+                scales=h_scales[grp][:],
                 in_=h_grouped[grp][:].rearrange("p g r t -> p (g r t)"),
             )
 
-        def project(j, block):
-            grp, jj = divmod(j, GROUP)
-            acc = psum_o.tile([P, N_TILE], F32, tag="acc")
+        def project(grp, jj, w, half):
+            n = len(GROUPS[grp])
+            acc = psum_o.tile([P, N_TILE], F32, name="acc", tag="acc")
             for g in range(PASSES):
-                h_cols = slice(
-                    (grp * PASSES + g) * GROUP_TOKENS + jj * P, (grp * PASSES + g) * GROUP_TOKENS + (jj + 1) * P
-                )
-                w_cols = slice((block * PASSES + g) * N_TILE, (block * PASSES + g + 1) * N_TILE)
+                h_cols = slice((g * n + jj) * P, (g * n + jj + 1) * P)
+                w_cols = slice(g * N_TILE, (g + 1) * N_TILE)
                 nc.tensor.matmul_mx(
                     out=acc[:],
-                    lhsT=h_codes[:, h_cols].bitcast(FP8X4),
-                    lhsT_scale=h_scales[:, h_cols],
-                    rhs=w_codes[:, w_cols].bitcast(FP8X4),
-                    rhs_scale=w_scales[:, w_cols],
+                    lhsT=h_codes[grp][:, h_cols].bitcast(FP8X4),
+                    lhsT_scale=h_scales[grp][:, h_cols],
+                    rhs=w_codes[w][half][:, w_cols].bitcast(FP8X4),
+                    rhs_scale=w_scales[w][half][:, w_cols],
                     start=(g == 0),
                     stop=(g == PASSES - 1),
                 )
             return acc
 
-        def store_keys(j, banks):
-            keys = stage.tile([P, FEATURES], F32, tag="keys")
-            for half in range(HALVES):
-                nc.scalar.copy(out=keys[:, half * N_TILE : (half + 1) * N_TILE], in_=banks[half][:])
-            nc.sync.dma_start(out=out_views[2][:, j, :], in_=keys[:])
-
+        keys = {}
         biased = {}
+        vals = {}
+        banks = {}
 
-        def add_biases(j, half, bank):
+        def queries(grp, jj, half):
+            banks[(grp, jj, half)] = project(grp, jj, 0, half)
+
+        def copy_keys(grp, jj, half):
+            j = GROUPS[grp][jj]
+            if half == 0:
+                keys[j] = stage.tile([P, FEATURES], F32, name="keys", tag="keys")
+            nc.scalar.copy(out=keys[j][:, half * N_TILE : (half + 1) * N_TILE], in_=banks[(grp, jj, half)][:])
+            if half == 1:
+                nc.sync.dma_start(out=out_views[2][:, j, :], in_=keys[j][:])
+
+        def add_biases(grp, jj, half):
+            j = GROUPS[grp][jj]
             if half == 0:
                 biased[j] = stage.tile([P, 2, FEATURES], F32, name="biased", tag="biased")
             cols = slice(half * N_TILE, (half + 1) * N_TILE)
             nc.vector.tensor_tensor(
                 out=biased[j][:, :, cols],
-                in0=bank[:].unsqueeze(1).to_broadcast([P, 2, N_TILE]),
+                in0=banks[(grp, jj, half)][:].unsqueeze(1).to_broadcast([P, 2, N_TILE]),
                 in1=bias_all[:, :, cols],
                 op=ALU.add,
             )
+            if half == 1:
+                nc.sync.dma_start(out=out_views[0][:, j, :], in_=biased[j][:, 0, :])
+                nc.sync.dma_start(out=out_views[1][:, j, :], in_=biased[j][:, 1, :])
 
-        def store_biased(j):
-            nc.sync.dma_start(out=out_views[0][:, j, :], in_=biased[j][:, 0, :])
-            nc.sync.dma_start(out=out_views[1][:, j, :], in_=biased[j][:, 1, :])
-
-        def values(j):
-            vals = stage.tile([P, FEATURES], F32, tag="vals")
+        def values(grp, jj):
+            j = GROUPS[grp][jj]
+            vals[j] = stage.tile([P, FEATURES], F32, name="vals", tag="vals")
             for half in range(HALVES):
-                acc = project(j, HALVES + half)
-                nc.scalar.copy(out=vals[:, half * N_TILE : (half + 1) * N_TILE], in_=acc[:])
-            nc.sync.dma_start(out=out_views[3][:, j, :], in_=vals[:])
+                acc = project(grp, jj, 1, half)
+                nc.scalar.copy(out=vals[j][:, half * N_TILE : (half + 1) * N_TILE], in_=acc[:])
+            nc.sync.dma_start(out=out_views[3][:, j, :], in_=vals[j][:])
 
-        def scalar_spare_time(slot):
-            if slot < HALVES * PASSES:
-                regroup_w(1, slot // PASSES, slot % PASSES, nc.scalar.copy)
-            else:
-                for j in range(GROUP * (slot - HALVES * PASSES), GROUP * (slot - HALVES * PASSES + 1)):
-                    if j < TOKEN_TILES:
-                        values(j)
-
-        token_statistics(0)
-        standard_deviation(0)
-        rows_to_columns()
-        regroup_w(0, 0, 0, nc.vector.tensor_copy)
-        normalise(0)
-        regroup_w(0, 1, 0, nc.scalar.copy)
-        transpose_and_scale(0)
-        spread_biases()
-        regroup_w(0, 0, 1, nc.vector.tensor_copy)
-        regroup_w(0, 1, 1, nc.vector.tensor_copy)
+        vector_copy = nc.vector.tensor_copy
+        scalar_copy = nc.scalar.copy
+        spread_bias(0, 0, scalar_copy)
+        spread_bias(1, 0, scalar_copy)
+        token_statistics(0, 0)
+        inverse_deviation(0)
+        minus_mean(0)
+        normalise(0, 0, ("scalar", "gpsimd"))
+        gamma_beta_columns()
+        token_statistics(1, 0)
+        inverse_deviation(1)
+        minus_mean(1)
+        regroup_w(0, 0, 0, 1, gpsimd_copy)
+        regroup_w(0, 0, 1, 1, gpsimd_copy)
+        regroup_w(0, 0, 0, 0, vector_copy)
+        transpose_and_scale(0, 0)
+        transpose_and_scale(0, 1)
+        regroup_w(0, 0, 1, 0, vector_copy)
+        regroup_h(0, 0, vector_copy)
+        regroup_h(0, 1, vector_copy)
         quantise_w(0, 0)
-        regroup_h(0)
-        quantise_w(0, 1)
         quantise_h(0)
-        scalar_spare_time(0)
-
-        for grp in range(GROUPS):
-            first, second = GROUP * grp, GROUP * grp + 1
-            more = grp + 1 < GROUPS
-            banks = {j: [project(j, half) for half in range(HALVES)] for j in (first, second)}
-            if more:
-                token_statistics(grp + 1)
-            store_keys(first, banks[first])
-            add_biases(first, 0, banks[first][0])
-            if more:
-                standard_deviation(grp + 1)
-                normalise(grp + 1)
-            store_keys(second, banks[second])
-            scalar_spare_time(2 * grp + 1)
-            add_biases(first, 1, banks[first][1])
-            store_biased(first)
-            add_biases(second, 0, banks[second][0])
-            add_biases(second, 1, banks[second][1])
-            store_biased(second)
-            if more:
-                transpose_and_scale(grp + 1)
-            if grp < HALVES:
-                quantise_w(1, grp)
-            scalar_spare_time(2 * grp + 2)
-            if more:
-                regroup_h(grp + 1)
+        queries(0, 0, 0)
+        normalise(1, 0, ("scalar", "scalar"))
+        regroup_w(0, 1, 0, 1, gpsimd_copy)
+        regroup_w(0, 1, 1, 1, gpsimd_copy)
+        regroup_w(0, 1, 0, 0, vector_copy)
+        regroup_w(0, 1, 1, 0, vector_copy)
+        copy_keys(0, 0, 0)
+        transpose_and_scale(1, 0)
+        transpose_and_scale(1, 1)
+        quantise_w(0, 1)
+        queries(0, 0, 1)
+        add_biases(0, 0, 0)
+        copy_keys(0, 0, 1)
+        spread_bias(0, 1, scalar_copy)
+        spread_bias(1, 1, scalar_copy)
+        regroup_h(1, 0, vector_copy)
+        regroup_h(1, 1, vector_copy)
+        quantise_h(1)
+        queries(1, 0, 0)
+        queries(1, 0, 1)
+        add_biases(0, 0, 1)
+        for g in range(PASSES):
+            for piece in range(N_TILE // W_PIECE):
+                regroup_w(1, 0, g, piece, gpsimd_copy)
+        copy_keys(1, 0, 0)
+        copy_keys(1, 0, 1)
+        add_biases(1, 0, 0)
+        token_statistics(2, 0)
+        token_statistics(2, 1)
+        inverse_deviation(2)
+        normalise(2, 0, ("gpsimd", "gpsimd"))
+        normalise(2, 1, ("gpsimd", "gpsimd"))
+        for g in range(PASSES):
+            for piece in range(N_TILE // W_PIECE):
+                regroup_w(1, 1, g, piece, scalar_copy)
+        add_biases(1, 0, 1)
+        quantise_w(1, 0)
+        token_statistics(3, 0)
+        token_statistics(3, 1)
+        inverse_deviation(3)
+        quantise_w(1, 1)
+        normalise(3, 0, ("gpsimd", "gpsimd"))
+        normalise(3, 1, ("gpsimd", "gpsimd"))
+        transpose_and_scale(2, 0)
+        transpose_and_scale(2, 1)
+        values(0, 0)
+        values(1, 0)
+        regroup_h(2, 0, vector_copy)
+        regroup_h(2, 1, vector_copy)
+        quantise_h(2)
+        for grp in range(2, len(GROUPS)):
+            nxt = grp + 1 < len(GROUPS)
+            nxt2 = grp + 2 < len(GROUPS)
+            queries(grp, 0, 0)
+            queries(grp, 0, 1)
+            copy_keys(grp, 0, 0)
+            copy_keys(grp, 0, 1)
+            add_biases(grp, 0, 0)
+            add_biases(grp, 0, 1)
+            if nxt:
+                transpose_and_scale(grp + 1, 0)
+            if nxt2:
+                token_statistics(grp + 2, 0)
+                token_statistics(grp + 2, 1)
+                inverse_deviation(grp + 2)
+                normalise(grp + 2, 0, ("gpsimd", "gpsimd"))
+                normalise(grp + 2, 1, ("gpsimd", "gpsimd"))
+            queries(grp, 1, 0)
+            queries(grp, 1, 1)
+            copy_keys(grp, 1, 0)
+            copy_keys(grp, 1, 1)
+            add_biases(grp, 1, 0)
+            if nxt:
+                transpose_and_scale(grp + 1, 1)
+                regroup_h(grp + 1, 0, vector_copy)
+            values(grp, 0)
+            add_biases(grp, 1, 1)
+            if nxt:
+                regroup_h(grp + 1, 1, vector_copy)
                 quantise_h(grp + 1)
+            values(grp, 1)

@@ -20,7 +20,7 @@ FEATURES = 1024
 PASSES = D_MODEL // K_PASS
 PLANES = PASSES * PACK
 TOKEN_TILES = TOKENS // P
-GROUPS = ((0,), (1,), (2, 3), (4, 5), (6, 7))
+GROUPS = ((0, 1), (2, 3), (4, 5), (6, 7))
 N_TILE = 512
 HALVES = FEATURES // N_TILE
 W_PIECE = 256
@@ -56,7 +56,6 @@ def tile_multiheadattentiowithrpe_pa_kernel(
         stage = ctx.enter_context(tc.tile_pool(name="stage", bufs=3))
         psum_t = ctx.enter_context(tc.psum_pool(name="psum_t", bufs=3))
         psum_o = ctx.enter_context(tc.psum_pool(name="psum_o", bufs=5))
-        ctx.enter_context(tc.manual_schedule())
 
         ident_bf = const.tile([P, P], BF16, name="ident_bf")
         make_identity(nc, ident_bf[:])
@@ -68,7 +67,7 @@ def tile_multiheadattentiowithrpe_pa_kernel(
         eps = const.tile([P, 1], F32, name="eps")
         nc.vector.memset(eps[:], EPS)
         warm = const.tile([P, 1], F32, name="warm")
-        nc.scalar.activation(out=warm[:], in_=eps[:], func=ACT.Abs_reciprocal_sqrt)
+        nc.scalar.activation(out=warm[:], in_=eps[:], func=ACT.Sqrt)
 
         x_sb = [
             keep.tile([P, len(tiles), D_MODEL], BF16, name="x_sb%d" % grp) for grp, tiles in enumerate(GROUPS)
@@ -85,29 +84,32 @@ def tile_multiheadattentiowithrpe_pa_kernel(
             tiles = GROUPS[grp]
             nc.sync.dma_start(out=x_sb[grp][:], in_=x_view[:, tiles[0] : tiles[-1] + 1, :])
 
+        def load_x_tile(grp, jj):
+            nc.sync.dma_start(out=x_sb[grp][:, jj, :], in_=x_view[:, GROUPS[grp][jj], :])
+
         def load_w(w, half):
             for g in range(PASSES):
                 nc.sync.dma_start(
                     out=w_raw[w][half][g][:], in_=w_views[w][g][:, :, half * N_TILE : (half + 1) * N_TILE]
                 )
 
-        load_x(0)
+        load_x_tile(0, 0)
+        load_x_tile(0, 1)
         for i, vec in enumerate((u_bias.rearrange("h f -> (h f)"), v_bias.rearrange("h f -> (h f)"), gamma, beta)):
             nc.sync.dma_start(out=rows[i : i + 1, :], in_=vec.unsqueeze(0))
-        load_x(1)
         load_w(0, 0)
         load_w(0, 1)
+        load_x(1)
         load_w(1, 0)
-        load_x(2)
         load_w(1, 1)
+        load_x(2)
         load_x(3)
-        load_x(4)
 
         gb_cols = const.tile([P, 2 * PLANES], F32, name="gb_cols")
         bias_all = const.tile([P, 2, FEATURES], F32, name="bias_all")
 
         def gamma_beta_columns():
-            cols_ps = psum_t.tile([P, PLANES, 2], F32, tag="xt")
+            cols_ps = psum_t.tile([P, PLANES, 2], F32, name="cols_ps", tag="xt")
             for g in range(PASSES):
                 for t in range(PACK):
                     nc.tensor.matmul(
@@ -121,16 +123,20 @@ def tile_multiheadattentiowithrpe_pa_kernel(
                 out=gb_cols[:].rearrange("p (v c) -> p v c", c=PLANES), in_=cols_ps[:].rearrange("p c v -> p v c")
             )
 
-        def spread_bias(b, half, copy):
-            bias_ps = psum_o.tile([P, N_TILE], F32, tag="acc")
+        bias_ps = {}
+
+        def spread_bias(b, half):
+            bias_ps[(b, half)] = psum_o.tile([P, N_TILE], F32, name="bias_ps", tag="acc")
             nc.tensor.matmul(
-                bias_ps[:],
+                bias_ps[(b, half)][:],
                 lhsT=ident_bf[:, b : b + 1].to_broadcast([P, P]),
                 rhs=rows[:, half * N_TILE : (half + 1) * N_TILE],
                 start=True,
                 stop=True,
             )
-            copy(out=bias_all[:, b, half * N_TILE : (half + 1) * N_TILE], in_=bias_ps[:])
+
+        def copy_bias(b, half):
+            nc.scalar.copy(out=bias_all[:, b, half * N_TILE : (half + 1) * N_TILE], in_=bias_ps[(b, half)][:])
 
         h_codes = [
             keep.tile([P, PASSES * len(tiles) * P], U32, name="h_codes%d" % grp, align_bytes=64)
@@ -174,6 +180,7 @@ def tile_multiheadattentiowithrpe_pa_kernel(
         mean_var = {}
         rstd = {}
         shift = {}
+        std = {}
         normed = {}
         h_planes = {}
         h_grouped = {}
@@ -189,12 +196,18 @@ def tile_multiheadattentiowithrpe_pa_kernel(
                 )
             nc.vector.bn_aggr(out=mean_var[grp][:, jj, :], in_=stats[:].rearrange("p s v -> p (s v)"))
 
+        def deviation(grp):
+            n = len(GROUPS[grp])
+            std[grp] = small.tile([P, n], F32, name="std", tag="std")
+            nc.scalar.activation(
+                out=std[grp][:], in_=mean_var[grp][:, :, 1], func=ACT.Sqrt, bias=eps[:, 0:1]
+            )
+
+
         def inverse_deviation(grp):
             n = len(GROUPS[grp])
             rstd[grp] = small.tile([P, n], F32, name="rstd", tag="rstd")
-            nc.scalar.activation(
-                out=rstd[grp][:], in_=mean_var[grp][:, :, 1], func=ACT.Abs_reciprocal_sqrt, bias=eps[:, 0:1]
-            )
+            nc.vector.reciprocal(out=rstd[grp][:], in_=std[grp][:])
 
         def minus_mean(grp):
             n = len(GROUPS[grp])
@@ -203,32 +216,29 @@ def tile_multiheadattentiowithrpe_pa_kernel(
                 out=shift[grp][:], in0=mean_var[grp][:, :, 0], scalar=-1.0, in1=rstd[grp][:], op0=ALU.mult, op1=ALU.mult
             )
 
-        def normalise(grp, jj, engines):
-            if jj == 0:
-                normed[grp] = []
-            xn = work.tile([P, D_MODEL], F32, name="xn", tag="xn", bufs=4)
-            for g in range(PASSES):
-                cols = slice(g * K_PASS, (g + 1) * K_PASS)
-                dst = xn[:, cols].rearrange("q (t p) -> q t p", t=PACK)
-                src = x_sb[grp][:, jj, cols].rearrange("q (p t) -> q t p", t=PACK)
-                if engines[g] == "scalar":
-                    nc.scalar.activation(
-                        out=dst,
-                        in_=src,
-                        func=ACT.Identity,
-                        scale=rstd[grp][:, jj : jj + 1],
-                        bias=shift[grp][:, jj : jj + 1],
-                    )
-                else:
-                    (nc.gpsimd if engines[g] == "gpsimd" else nc.vector).tensor_scalar(
-                        out=dst,
-                        in0=src,
-                        scalar1=mean_var[grp][:, jj, 0:1],
-                        scalar2=rstd[grp][:, jj : jj + 1],
-                        op0=ALU.subtract,
-                        op1=ALU.mult,
-                    )
-            normed[grp].append(xn)
+        def normalise(grp, jj, g, engine):
+            if g == 0:
+                normed[(grp, jj)] = work.tile([P, D_MODEL], F32, name="xn", tag="xn", bufs=4)
+            cols = slice(g * K_PASS, (g + 1) * K_PASS)
+            dst = normed[(grp, jj)][:, cols].rearrange("q (t p) -> q t p", t=PACK)
+            src = x_sb[grp][:, jj, cols].rearrange("q (p t) -> q t p", t=PACK)
+            if engine is nc.scalar:
+                nc.scalar.activation(
+                    out=dst,
+                    in_=src,
+                    func=ACT.Identity,
+                    scale=rstd[grp][:, jj : jj + 1],
+                    bias=shift[grp][:, jj : jj + 1],
+                )
+            else:
+                engine.tensor_scalar(
+                    out=dst,
+                    in0=src,
+                    scalar1=mean_var[grp][:, jj, 0:1],
+                    scalar2=rstd[grp][:, jj : jj + 1],
+                    op0=ALU.subtract,
+                    op1=ALU.mult,
+                )
 
         def transpose_and_scale(grp, g):
             n = len(GROUPS[grp])
@@ -241,7 +251,7 @@ def tile_multiheadattentiowithrpe_pa_kernel(
                     c = c0 + cc
                     for jj in range(n):
                         nc.tensor.transpose(
-                            xt[:, cc, jj * P : (jj + 1) * P], normed[grp][jj][:, c * P : (c + 1) * P], ident[:]
+                            xt[:, cc, jj * P : (jj + 1) * P], normed[(grp, jj)][:, c * P : (c + 1) * P], ident[:]
                         )
                 for cc in range(per_bank):
                     c = c0 + cc
@@ -289,144 +299,169 @@ def tile_multiheadattentiowithrpe_pa_kernel(
             return acc
 
         keys = {}
-        biased = {}
+        halves_done = set()
+        with_u = {}
+        with_v = {}
         vals = {}
         banks = {}
 
         def queries(grp, jj, half):
             banks[(grp, jj, half)] = project(grp, jj, 0, half)
 
-        def copy_keys(grp, jj, half):
+        def store(o, j, tile, half, split):
+            if split:
+                cols = slice(half * N_TILE, (half + 1) * N_TILE)
+                nc.sync.dma_start(out=out_views[o][:, j, cols], in_=tile[:, cols])
+            elif (o, j) in halves_done:
+                nc.sync.dma_start(out=out_views[o][:, j, :], in_=tile[:])
+            halves_done.add((o, j))
+
+        def copy_keys(grp, jj, half, split=False):
             j = GROUPS[grp][jj]
-            if half == 0:
+            if j not in keys:
                 keys[j] = stage.tile([P, FEATURES], F32, name="keys", tag="keys")
             nc.scalar.copy(out=keys[j][:, half * N_TILE : (half + 1) * N_TILE], in_=banks[(grp, jj, half)][:])
-            if half == 1:
-                nc.sync.dma_start(out=out_views[2][:, j, :], in_=keys[j][:])
+            store(2, j, keys[j], half, split)
 
-        def add_biases(grp, jj, half):
+        def add_u(grp, jj, half, split=False):
             j = GROUPS[grp][jj]
-            if half == 0:
-                biased[j] = stage.tile([P, 2, FEATURES], F32, name="biased", tag="biased")
+            if j not in with_u:
+                with_u[j] = stage.tile([P, FEATURES], F32, name="with_u", tag="with_u")
             cols = slice(half * N_TILE, (half + 1) * N_TILE)
             nc.vector.tensor_tensor(
-                out=biased[j][:, :, cols],
-                in0=banks[(grp, jj, half)][:].unsqueeze(1).to_broadcast([P, 2, N_TILE]),
-                in1=bias_all[:, :, cols],
-                op=ALU.add,
+                out=with_u[j][:, cols], in0=banks[(grp, jj, half)][:], in1=bias_all[:, 0, cols], op=ALU.add
             )
-            if half == 1:
-                nc.sync.dma_start(out=out_views[0][:, j, :], in_=biased[j][:, 0, :])
-                nc.sync.dma_start(out=out_views[1][:, j, :], in_=biased[j][:, 1, :])
+            store(0, j, with_u[j], half, split)
 
-        def values(grp, jj):
+        def add_v(grp, jj, half, engine, split=False):
             j = GROUPS[grp][jj]
-            vals[j] = stage.tile([P, FEATURES], F32, name="vals", tag="vals")
-            for half in range(HALVES):
-                acc = project(grp, jj, 1, half)
-                nc.scalar.copy(out=vals[j][:, half * N_TILE : (half + 1) * N_TILE], in_=acc[:])
-            nc.sync.dma_start(out=out_views[3][:, j, :], in_=vals[j][:])
+            if j not in with_v:
+                with_v[j] = stage.tile([P, FEATURES], F32, name="with_v", tag="with_v")
+            cols = slice(half * N_TILE, (half + 1) * N_TILE)
+            src = keys[j][:, cols] if engine is nc.gpsimd else banks[(grp, jj, half)][:]
+            engine.tensor_tensor(out=with_v[j][:, cols], in0=src, in1=bias_all[:, 1, cols], op=ALU.add)
+            store(1, j, with_v[j], half, split)
+
+        def values(grp, jj, half, split=False):
+            j = GROUPS[grp][jj]
+            if j not in vals:
+                vals[j] = stage.tile([P, FEATURES], F32, name="vals", tag="vals")
+            acc = project(grp, jj, 1, half)
+            nc.scalar.copy(out=vals[j][:, half * N_TILE : (half + 1) * N_TILE], in_=acc[:])
+            store(3, j, vals[j], half, split)
 
         vector_copy = nc.vector.tensor_copy
         scalar_copy = nc.scalar.copy
-        spread_bias(0, 0, scalar_copy)
-        spread_bias(1, 0, scalar_copy)
+        V, S, G = nc.vector, nc.scalar, nc.gpsimd
+        for half in range(HALVES):
+            spread_bias(0, half)
+            spread_bias(1, half)
+        copy_bias(0, 0)
+        copy_bias(1, 0)
         token_statistics(0, 0)
+        token_statistics(0, 1)
+        deviation(0)
         inverse_deviation(0)
-        minus_mean(0)
-        normalise(0, 0, ("scalar", "gpsimd"))
+        normalise(0, 0, 0, V)
+        normalise(0, 1, 0, V)
         gamma_beta_columns()
-        token_statistics(1, 0)
-        inverse_deviation(1)
-        minus_mean(1)
-        regroup_w(0, 0, 0, 1, gpsimd_copy)
-        regroup_w(0, 0, 1, 1, gpsimd_copy)
-        regroup_w(0, 0, 0, 0, vector_copy)
+        regroup_w(0, 0, 0, 0, scalar_copy)
+        regroup_w(0, 0, 0, 1, vector_copy)
+        normalise(0, 0, 1, V)
+        normalise(0, 1, 1, V)
+        regroup_w(0, 0, 1, 0, vector_copy)
+        regroup_w(0, 0, 1, 1, vector_copy)
         transpose_and_scale(0, 0)
         transpose_and_scale(0, 1)
-        regroup_w(0, 0, 1, 0, vector_copy)
+        copy_bias(0, 1)
+        copy_bias(1, 1)
         regroup_h(0, 0, vector_copy)
-        regroup_h(0, 1, vector_copy)
         quantise_w(0, 0)
+        regroup_h(0, 1, vector_copy)
         quantise_h(0)
         queries(0, 0, 0)
-        normalise(1, 0, ("scalar", "scalar"))
-        regroup_w(0, 1, 0, 1, gpsimd_copy)
-        regroup_w(0, 1, 1, 1, gpsimd_copy)
-        regroup_w(0, 1, 0, 0, vector_copy)
+        queries(0, 1, 0)
+        regroup_w(0, 1, 0, 0, scalar_copy)
+        regroup_w(0, 1, 0, 1, scalar_copy)
         regroup_w(0, 1, 1, 0, vector_copy)
-        copy_keys(0, 0, 0)
+        regroup_w(0, 1, 1, 1, vector_copy)
+        copy_keys(0, 0, 0, True)
+        add_v(0, 0, 0, G, True)
+        add_u(0, 0, 0, True)
+        quantise_w(0, 1)
+        copy_keys(0, 1, 0, True)
+        add_v(0, 1, 0, G, True)
+        add_u(0, 1, 0, True)
+        token_statistics(1, 0)
+        queries(0, 0, 1)
+        queries(0, 1, 1)
+        regroup_w(1, 0, 0, 0, scalar_copy)
+        copy_keys(0, 0, 1, True)
+        add_v(0, 0, 1, G, True)
+        copy_keys(0, 1, 1, True)
+        add_v(0, 1, 1, G, True)
+        token_statistics(1, 1)
+        deviation(1)
+        add_u(0, 0, 1, True)
+        add_u(0, 1, 1, True)
+        inverse_deviation(1)
+        regroup_w(1, 0, 0, 1, scalar_copy)
+        for g in range(PASSES):
+            normalise(1, 0, g, V)
+            normalise(1, 1, g, V)
         transpose_and_scale(1, 0)
         transpose_and_scale(1, 1)
-        quantise_w(0, 1)
-        queries(0, 0, 1)
-        add_biases(0, 0, 0)
-        copy_keys(0, 0, 1)
-        spread_bias(0, 1, scalar_copy)
-        spread_bias(1, 1, scalar_copy)
+        token_statistics(2, 0)
         regroup_h(1, 0, vector_copy)
         regroup_h(1, 1, vector_copy)
         quantise_h(1)
-        queries(1, 0, 0)
-        queries(1, 0, 1)
-        add_biases(0, 0, 1)
-        for g in range(PASSES):
-            for piece in range(N_TILE // W_PIECE):
-                regroup_w(1, 0, g, piece, gpsimd_copy)
-        copy_keys(1, 0, 0)
-        copy_keys(1, 0, 1)
-        add_biases(1, 0, 0)
-        token_statistics(2, 0)
-        token_statistics(2, 1)
-        inverse_deviation(2)
-        normalise(2, 0, ("gpsimd", "gpsimd"))
-        normalise(2, 1, ("gpsimd", "gpsimd"))
-        for g in range(PASSES):
-            for piece in range(N_TILE // W_PIECE):
-                regroup_w(1, 1, g, piece, scalar_copy)
-        add_biases(1, 0, 1)
-        quantise_w(1, 0)
-        token_statistics(3, 0)
-        token_statistics(3, 1)
-        inverse_deviation(3)
-        quantise_w(1, 1)
-        normalise(3, 0, ("gpsimd", "gpsimd"))
-        normalise(3, 1, ("gpsimd", "gpsimd"))
-        transpose_and_scale(2, 0)
-        transpose_and_scale(2, 1)
-        values(0, 0)
-        values(1, 0)
-        regroup_h(2, 0, vector_copy)
-        regroup_h(2, 1, vector_copy)
-        quantise_h(2)
-        for grp in range(2, len(GROUPS)):
-            nxt = grp + 1 < len(GROUPS)
-            nxt2 = grp + 2 < len(GROUPS)
-            queries(grp, 0, 0)
-            queries(grp, 0, 1)
-            copy_keys(grp, 0, 0)
-            copy_keys(grp, 0, 1)
-            add_biases(grp, 0, 0)
-            add_biases(grp, 0, 1)
-            if nxt:
+        regroup_w(1, 0, 1, 0, scalar_copy)
+        for grp in range(1, len(GROUPS)):
+            more = grp + 1 < len(GROUPS)
+            for jj in range(2):
+                for half in range(HALVES):
+                    queries(grp, jj, half)
+            if more:
+                token_statistics(grp + 1, 1)
+                deviation(grp + 1)
+            if grp == 1:
+                regroup_w(1, 0, 1, 1, scalar_copy)
+            for jj in range(2):
+                for half in range(HALVES):
+                    copy_keys(grp, jj, half)
+                    add_u(grp, jj, half)
+                    add_v(grp, jj, half, G if more or jj == 0 else V)
+                if jj == 0 and grp > 1:
+                    values(grp, 0, 0)
+                    values(grp, 0, 1)
+                if jj == 0 and more:
+                    inverse_deviation(grp + 1)
+                    for g in range(PASSES):
+                        normalise(grp + 1, 0, g, V)
+                        normalise(grp + 1, 1, g, V)
+                if jj == 0 and grp == 1:
+                    quantise_w(1, 0)
+                    regroup_w(1, 1, 0, 0, vector_copy)
+                    regroup_w(1, 1, 0, 1, vector_copy)
+            if more:
                 transpose_and_scale(grp + 1, 0)
-            if nxt2:
-                token_statistics(grp + 2, 0)
-                token_statistics(grp + 2, 1)
-                inverse_deviation(grp + 2)
-                normalise(grp + 2, 0, ("gpsimd", "gpsimd"))
-                normalise(grp + 2, 1, ("gpsimd", "gpsimd"))
-            queries(grp, 1, 0)
-            queries(grp, 1, 1)
-            copy_keys(grp, 1, 0)
-            copy_keys(grp, 1, 1)
-            add_biases(grp, 1, 0)
-            if nxt:
                 transpose_and_scale(grp + 1, 1)
+            if grp == 1:
+                regroup_w(1, 1, 1, 0, scalar_copy)
+                regroup_w(1, 1, 1, 1, scalar_copy)
+                values(0, 0, 0)
+                values(0, 1, 0)
+            if more:
                 regroup_h(grp + 1, 0, vector_copy)
-            values(grp, 0)
-            add_biases(grp, 1, 1)
-            if nxt:
+                if grp + 2 < len(GROUPS):
+                    token_statistics(grp + 2, 0)
                 regroup_h(grp + 1, 1, vector_copy)
                 quantise_h(grp + 1)
-            values(grp, 1)
+            if grp == 1:
+                quantise_w(1, 1)
+                values(0, 0, 1)
+                values(0, 1, 1)
+                values(1, 0, 0)
+                values(1, 0, 1)
+            values(grp, 1, 0)
+            values(grp, 1, 1)

@@ -62,7 +62,7 @@ def tile_multiheadattentiowithrpe_pa_kernel(
         ident = const.tile([P, P], F32, name="ident")
         make_identity(nc, ident[:])
 
-        rows = const.tile([P, FEATURES], BF16, name="rows")
+        rows = const.tile([P, N_TILE], BF16, name="rows")
         nc.vector.memset(rows[:], 0.0)
         eps = const.tile([P, 1], F32, name="eps")
         nc.vector.memset(eps[:], EPS)
@@ -73,11 +73,7 @@ def tile_multiheadattentiowithrpe_pa_kernel(
             keep.tile([P, len(tiles), D_MODEL], BF16, name="x_sb%d" % grp) for grp, tiles in enumerate(GROUPS)
         ]
         w_raw = [
-            [
-                [keep.tile([P, PACK, N_TILE], BF16, name="w_raw%d%d%d" % (w, half, g)) for g in range(PASSES)]
-                for half in range(HALVES)
-            ]
-            for w in range(2)
+            [keep.tile([P, PACK, FEATURES], BF16, name="w_raw%d%d" % (w, g)) for g in range(PASSES)] for w in range(2)
         ]
 
         def load_x(grp):
@@ -87,21 +83,17 @@ def tile_multiheadattentiowithrpe_pa_kernel(
         def load_x_tile(grp, jj):
             nc.sync.dma_start(out=x_sb[grp][:, jj, :], in_=x_view[:, GROUPS[grp][jj], :])
 
-        def load_w(w, half):
+        def load_w(w):
             for g in range(PASSES):
-                nc.sync.dma_start(
-                    out=w_raw[w][half][g][:], in_=w_views[w][g][:, :, half * N_TILE : (half + 1) * N_TILE]
-                )
+                nc.sync.dma_start(out=w_raw[w][g][:], in_=w_views[w][g])
 
         load_x_tile(0, 0)
         load_x_tile(0, 1)
         for i, vec in enumerate((u_bias.rearrange("h f -> (h f)"), v_bias.rearrange("h f -> (h f)"), gamma, beta)):
-            nc.sync.dma_start(out=rows[i : i + 1, :], in_=vec.unsqueeze(0))
-        load_w(0, 0)
-        load_w(0, 1)
+            nc.sync.dma_start(out=rows[2 * i : 2 * i + 2, :], in_=vec.rearrange("(r n) -> r n", n=N_TILE))
+        load_w(0)
         load_x(1)
-        load_w(1, 0)
-        load_w(1, 1)
+        load_w(1)
         load_x(2)
         load_x(3)
 
@@ -109,18 +101,13 @@ def tile_multiheadattentiowithrpe_pa_kernel(
         bias_all = const.tile([P, 2, FEATURES], F32, name="bias_all")
 
         def gamma_beta_columns():
-            cols_ps = psum_t.tile([P, PLANES, 2], F32, name="cols_ps", tag="xt")
-            for g in range(PASSES):
-                for t in range(PACK):
-                    nc.tensor.matmul(
-                        cols_ps[:, g * PACK + t, :],
-                        lhsT=rows[:, g * K_PASS + t : (g + 1) * K_PASS : PACK],
-                        rhs=ident_bf[:, 2:4],
-                        start=True,
-                        stop=True,
-                    )
+            cols_ps = psum_t.tile([P, PACK, 4], F32, name="cols_ps", tag="xt")
+            for t in range(PACK):
+                nc.tensor.matmul(
+                    cols_ps[:, t, :], lhsT=rows[:, t:N_TILE:PACK], rhs=ident_bf[:, 4:8], start=True, stop=True
+                )
             nc.vector.tensor_copy(
-                out=gb_cols[:].rearrange("p (v c) -> p v c", c=PLANES), in_=cols_ps[:].rearrange("p c v -> p v c")
+                out=gb_cols[:].rearrange("p (r t) -> p r t", t=PACK), in_=cols_ps[:].rearrange("p t r -> p r t")
             )
 
         bias_ps = {}
@@ -129,8 +116,8 @@ def tile_multiheadattentiowithrpe_pa_kernel(
             bias_ps[(b, half)] = psum_o.tile([P, N_TILE], F32, name="bias_ps", tag="acc")
             nc.tensor.matmul(
                 bias_ps[(b, half)][:],
-                lhsT=ident_bf[:, b : b + 1].to_broadcast([P, P]),
-                rhs=rows[:, half * N_TILE : (half + 1) * N_TILE],
+                lhsT=ident_bf[:, 2 * b + half : 2 * b + half + 1].to_broadcast([P, P]),
+                rhs=rows[:],
                 start=True,
                 stop=True,
             )
@@ -166,8 +153,11 @@ def tile_multiheadattentiowithrpe_pa_kernel(
             nc.gpsimd.tensor_scalar(out=out, in0=in_, scalar1=1.0, scalar2=0.0, op0=ALU.mult, op1=ALU.add)
 
         def regroup_w(w, half, g, piece, copy):
-            cols = slice(piece * W_PIECE, (piece + 1) * W_PIECE)
-            dst, src = regroup_views(w_grouped[w][half][:, g, cols, :], w_raw[w][half][g][:, :, cols])
+            c0 = piece * W_PIECE
+            n0 = half * N_TILE + c0
+            dst, src = regroup_views(
+                w_grouped[w][half][:, g, c0 : c0 + W_PIECE, :], w_raw[w][g][:, :, n0 : n0 + W_PIECE]
+            )
             copy(out=dst, in_=src)
 
         def quantise_w(w, half):
@@ -353,115 +343,142 @@ def tile_multiheadattentiowithrpe_pa_kernel(
         vector_copy = nc.vector.tensor_copy
         scalar_copy = nc.scalar.copy
         V, S, G = nc.vector, nc.scalar, nc.gpsimd
-        for half in range(HALVES):
-            spread_bias(0, half)
-            spread_bias(1, half)
-        copy_bias(0, 0)
-        copy_bias(1, 0)
-        token_statistics(0, 0)
-        token_statistics(0, 1)
-        deviation(0)
-        inverse_deviation(0)
-        normalise(0, 0, 0, V)
-        normalise(0, 1, 0, V)
-        gamma_beta_columns()
-        regroup_w(0, 0, 0, 0, scalar_copy)
-        regroup_w(0, 0, 0, 1, vector_copy)
-        normalise(0, 0, 1, V)
-        normalise(0, 1, 1, V)
-        regroup_w(0, 0, 1, 0, vector_copy)
-        regroup_w(0, 0, 1, 1, vector_copy)
-        transpose_and_scale(0, 0)
-        transpose_and_scale(0, 1)
-        copy_bias(0, 1)
-        copy_bias(1, 1)
-        regroup_h(0, 0, vector_copy)
-        quantise_w(0, 0)
-        regroup_h(0, 1, vector_copy)
-        quantise_h(0)
-        queries(0, 0, 0)
-        queries(0, 1, 0)
-        regroup_w(0, 1, 0, 0, scalar_copy)
-        regroup_w(0, 1, 0, 1, scalar_copy)
-        regroup_w(0, 1, 1, 0, vector_copy)
-        regroup_w(0, 1, 1, 1, vector_copy)
-        copy_keys(0, 0, 0, True)
-        add_v(0, 0, 0, G, True)
-        add_u(0, 0, 0, True)
-        quantise_w(0, 1)
-        copy_keys(0, 1, 0, True)
+        with tc.manual_schedule():
+            token_statistics(0, 0)
+            token_statistics(0, 1)
+            gamma_beta_columns()
+            spread_bias(0, 0)
+            spread_bias(1, 0)
+            spread_bias(0, 1)
+            spread_bias(1, 1)
+            copy_bias(0, 0)
+            deviation(0)
+            inverse_deviation(0)
+            normalise(0, 0, 0, V)
+            normalise(0, 1, 0, V)
+            regroup_w(0, 0, 0, 0, scalar_copy)
+            regroup_w(0, 0, 0, 1, vector_copy)
+            normalise(0, 0, 1, V)
+            normalise(0, 1, 1, V)
+            regroup_w(0, 0, 1, 0, vector_copy)
+            regroup_w(0, 0, 1, 1, vector_copy)
+            transpose_and_scale(0, 0)
+            transpose_and_scale(0, 1)
+            regroup_h(0, 0, vector_copy)
+            quantise_w(0, 0)
+            regroup_h(0, 1, vector_copy)
+            quantise_h(0)
+            regroup_w(0, 1, 0, 0, scalar_copy)
+            regroup_w(0, 1, 0, 1, scalar_copy)
+            queries(0, 0, 0)
+            queries(0, 1, 0)
+            regroup_w(0, 1, 1, 0, vector_copy)
+            regroup_w(0, 1, 1, 1, vector_copy)
+            copy_bias(1, 0)
+            add_u(0, 0, 0, True)
+            copy_keys(0, 1, 0, True)
+            quantise_w(0, 1)
+            copy_keys(0, 0, 0, True)
         add_v(0, 1, 0, G, True)
+        add_v(0, 0, 0, G, True)
         add_u(0, 1, 0, True)
         token_statistics(1, 0)
-        queries(0, 0, 1)
-        queries(0, 1, 1)
-        regroup_w(1, 0, 0, 0, scalar_copy)
-        copy_keys(0, 0, 1, True)
-        add_v(0, 0, 1, G, True)
-        copy_keys(0, 1, 1, True)
-        add_v(0, 1, 1, G, True)
         token_statistics(1, 1)
         deviation(1)
-        add_u(0, 0, 1, True)
-        add_u(0, 1, 1, True)
         inverse_deviation(1)
-        regroup_w(1, 0, 0, 1, scalar_copy)
         for g in range(PASSES):
             normalise(1, 0, g, V)
             normalise(1, 1, g, V)
+        copy_bias(0, 1)
+        copy_bias(1, 1)
+        queries(0, 0, 1)
+        queries(0, 1, 1)
+        for jj in range(2):
+            copy_keys(0, jj, 1, True)
+            add_u(0, jj, 1, True)
+            add_v(0, jj, 1, G, True)
         transpose_and_scale(1, 0)
         transpose_and_scale(1, 1)
-        token_statistics(2, 0)
         regroup_h(1, 0, vector_copy)
         regroup_h(1, 1, vector_copy)
         quantise_h(1)
+        regroup_w(1, 0, 0, 0, scalar_copy)
+        regroup_w(1, 0, 0, 1, scalar_copy)
         regroup_w(1, 0, 1, 0, scalar_copy)
-        for grp in range(1, len(GROUPS)):
-            more = grp + 1 < len(GROUPS)
-            for jj in range(2):
-                for half in range(HALVES):
-                    queries(grp, jj, half)
-            if more:
-                token_statistics(grp + 1, 1)
-                deviation(grp + 1)
-            if grp == 1:
-                regroup_w(1, 0, 1, 1, scalar_copy)
-            for jj in range(2):
-                for half in range(HALVES):
-                    copy_keys(grp, jj, half)
-                    add_u(grp, jj, half)
-                    add_v(grp, jj, half, G if more or jj == 0 else V)
-                if jj == 0 and grp > 1:
-                    values(grp, 0, 0)
-                    values(grp, 0, 1)
-                if jj == 0 and more:
-                    inverse_deviation(grp + 1)
-                    for g in range(PASSES):
-                        normalise(grp + 1, 0, g, V)
-                        normalise(grp + 1, 1, g, V)
-                if jj == 0 and grp == 1:
-                    quantise_w(1, 0)
-                    regroup_w(1, 1, 0, 0, vector_copy)
-                    regroup_w(1, 1, 0, 1, vector_copy)
-            if more:
-                transpose_and_scale(grp + 1, 0)
-                transpose_and_scale(grp + 1, 1)
-            if grp == 1:
-                regroup_w(1, 1, 1, 0, scalar_copy)
-                regroup_w(1, 1, 1, 1, scalar_copy)
-                values(0, 0, 0)
-                values(0, 1, 0)
-            if more:
-                regroup_h(grp + 1, 0, vector_copy)
-                if grp + 2 < len(GROUPS):
-                    token_statistics(grp + 2, 0)
-                regroup_h(grp + 1, 1, vector_copy)
-                quantise_h(grp + 1)
-            if grp == 1:
-                quantise_w(1, 1)
-                values(0, 0, 1)
-                values(0, 1, 1)
-                values(1, 0, 0)
-                values(1, 0, 1)
-            values(grp, 1, 0)
-            values(grp, 1, 1)
+        regroup_w(1, 0, 1, 1, scalar_copy)
+        quantise_w(1, 0)
+        values(0, 0, 0, True)
+        values(0, 1, 0, True)
+        regroup_w(1, 1, 0, 0, vector_copy)
+        regroup_w(1, 1, 0, 1, vector_copy)
+        regroup_w(1, 1, 1, 0, scalar_copy)
+        regroup_w(1, 1, 1, 1, scalar_copy)
+        quantise_w(1, 1)
+        values(0, 0, 1, True)
+        values(0, 1, 1, True)
+        token_statistics(2, 0)
+        token_statistics(2, 1)
+        deviation(2)
+        inverse_deviation(2)
+        for g in range(PASSES):
+            normalise(2, 0, g, V)
+            normalise(2, 1, g, V)
+        for half in range(HALVES):
+            queries(1, 0, half)
+            copy_keys(1, 0, half)
+            add_u(1, 0, half)
+            add_v(1, 0, half, G)
+        for half in range(HALVES):
+            queries(1, 1, half)
+            copy_keys(1, 1, half)
+            add_u(1, 1, half)
+            add_v(1, 1, half, G)
+        transpose_and_scale(2, 0)
+        transpose_and_scale(2, 1)
+        regroup_h(2, 0, vector_copy)
+        regroup_h(2, 1, vector_copy)
+        quantise_h(2)
+        values(1, 0, 0)
+        values(1, 0, 1)
+        values(1, 1, 0)
+        values(1, 1, 1)
+        token_statistics(3, 0)
+        token_statistics(3, 1)
+        deviation(3)
+        inverse_deviation(3)
+        for g in range(PASSES):
+            normalise(3, 0, g, V)
+            normalise(3, 1, g, V)
+        for half in range(HALVES):
+            queries(2, 0, half)
+            copy_keys(2, 0, half)
+            add_u(2, 0, half)
+            add_v(2, 0, half, G)
+        values(2, 0, 0)
+        values(2, 0, 1)
+        transpose_and_scale(3, 0)
+        transpose_and_scale(3, 1)
+        regroup_h(3, 0, vector_copy)
+        regroup_h(3, 1, vector_copy)
+        quantise_h(3)
+        for half in range(HALVES):
+            queries(2, 1, half)
+            copy_keys(2, 1, half)
+            add_u(2, 1, half)
+            add_v(2, 1, half, G)
+        values(2, 1, 0)
+        values(2, 1, 1)
+        for half in range(HALVES):
+            queries(3, 0, half)
+            copy_keys(3, 0, half)
+            add_u(3, 0, half)
+            add_v(3, 0, half, G)
+        values(3, 0, 0)
+        values(3, 0, 1)
+        for half in range(HALVES):
+            queries(3, 1, half)
+            copy_keys(3, 1, half)
+            add_u(3, 1, half)
+            add_v(3, 1, half, V)
+        values(3, 1, 0)
+        values(3, 1, 1)

@@ -20,12 +20,14 @@ FEATURES = 1024
 PASSES = D_MODEL // K_PASS
 PLANES = PASSES * PACK
 TOKEN_TILES = TOKENS // P
-GROUPS = ((0, 1), (2, 3), (4, 5), (6, 7))
+GROUPS = ((0, 1), (2,), (3,), (4,), (5,), (6,), (7,))
+EARLY_GROUPS = 3
 N_TILE = 512
 HALVES = FEATURES // N_TILE
 W_PIECE = 256
 BN_WIDTH = 512
 EPS = 1e-5
+V_PIECE = 256
 
 FLOPS = 2 * TOKENS * D_MODEL * 2 * FEATURES
 
@@ -92,10 +94,11 @@ def tile_multiheadattentiowithrpe_pa_kernel(
         for i, vec in enumerate((u_bias.rearrange("h f -> (h f)"), v_bias.rearrange("h f -> (h f)"), gamma, beta)):
             nc.sync.dma_start(out=rows[2 * i : 2 * i + 2, :], in_=vec.rearrange("(r n) -> r n", n=N_TILE))
         load_w(0)
-        load_x(1)
+        for grp in range(1, EARLY_GROUPS):
+            load_x(grp)
         load_w(1)
-        load_x(2)
-        load_x(3)
+        for grp in range(EARLY_GROUPS, len(GROUPS)):
+            load_x(grp)
 
         gb_cols = const.tile([P, 2 * PLANES], F32, name="gb_cols")
         bias_all = const.tile([P, 2, FEATURES], F32, name="bias_all")
@@ -152,19 +155,18 @@ def tile_multiheadattentiowithrpe_pa_kernel(
         def gpsimd_copy(out, in_):
             nc.gpsimd.tensor_scalar(out=out, in0=in_, scalar1=1.0, scalar2=0.0, op0=ALU.mult, op1=ALU.add)
 
-        def regroup_w(w, half, g, piece, copy):
-            c0 = piece * W_PIECE
+        def regroup_w(w, half, g, piece, copy, width=W_PIECE):
+            c0 = piece * width
             n0 = half * N_TILE + c0
-            dst, src = regroup_views(
-                w_grouped[w][half][:, g, c0 : c0 + W_PIECE, :], w_raw[w][g][:, :, n0 : n0 + W_PIECE]
-            )
+            dst, src = regroup_views(w_grouped[w][half][:, g, c0 : c0 + width, :], w_raw[w][g][:, :, n0 : n0 + width])
             copy(out=dst, in_=src)
 
-        def quantise_w(w, half):
+        def quantise_w(w, half, passes=PASSES, first=0):
+            cols = slice(first * N_TILE, (first + passes) * N_TILE)
             nc.vector.quantize_mx(
-                out=w_codes[w][half][:].bitcast(FP8X4),
-                scales=w_scales[w][half][:],
-                in_=w_grouped[w][half][:].rearrange("p g n t -> p (g n t)"),
+                out=w_codes[w][half][:, cols].bitcast(FP8X4),
+                scales=w_scales[w][half][:, cols],
+                in_=w_grouped[w][half][:, first : first + passes, :, :].rearrange("p g n t -> p (g n t)"),
             )
 
         mean_var = {}
@@ -186,18 +188,21 @@ def tile_multiheadattentiowithrpe_pa_kernel(
                 )
             nc.vector.bn_aggr(out=mean_var[grp][:, jj, :], in_=stats[:].rearrange("p s v -> p (s v)"))
 
-        def deviation(grp):
+        def deviation(grp, jj=None):
             n = len(GROUPS[grp])
-            std[grp] = small.tile([P, n], F32, name="std", tag="std")
+            if grp not in std:
+                std[grp] = small.tile([P, n], F32, name="std", tag="std")
+            cols = slice(0, n) if jj is None else slice(jj, jj + 1)
             nc.scalar.activation(
-                out=std[grp][:], in_=mean_var[grp][:, :, 1], func=ACT.Sqrt, bias=eps[:, 0:1]
+                out=std[grp][:, cols], in_=mean_var[grp][:, cols, 1], func=ACT.Sqrt, bias=eps[:, 0:1]
             )
 
-
-        def inverse_deviation(grp):
+        def inverse_deviation(grp, jj=None):
             n = len(GROUPS[grp])
-            rstd[grp] = small.tile([P, n], F32, name="rstd", tag="rstd")
-            nc.vector.reciprocal(out=rstd[grp][:], in_=std[grp][:])
+            if grp not in rstd:
+                rstd[grp] = small.tile([P, n], F32, name="rstd", tag="rstd")
+            cols = slice(0, n) if jj is None else slice(jj, jj + 1)
+            nc.vector.reciprocal(out=rstd[grp][:, cols], in_=std[grp][:, cols])
 
         def minus_mean(grp):
             n = len(GROUPS[grp])
@@ -327,9 +332,10 @@ def tile_multiheadattentiowithrpe_pa_kernel(
             j = GROUPS[grp][jj]
             if j not in with_v:
                 with_v[j] = stage.tile([P, FEATURES], F32, name="with_v", tag="with_v")
-            cols = slice(half * N_TILE, (half + 1) * N_TILE)
-            src = keys[j][:, cols] if engine is nc.gpsimd else banks[(grp, jj, half)][:]
-            engine.tensor_tensor(out=with_v[j][:, cols], in0=src, in1=bias_all[:, 1, cols], op=ALU.add)
+            for c0 in range(half * N_TILE, (half + 1) * N_TILE, V_PIECE):
+                piece = slice(c0, c0 + V_PIECE)
+                src = keys[j][:, piece] if engine is nc.gpsimd else banks[(grp, jj, half)][:, c0 - half * N_TILE : c0 - half * N_TILE + V_PIECE]
+                engine.tensor_tensor(out=with_v[j][:, piece], in0=src, in1=bias_all[:, 1, piece], op=ALU.add)
             store(1, j, with_v[j], half, split)
 
         def values(grp, jj, half, split=False):
@@ -345,58 +351,62 @@ def tile_multiheadattentiowithrpe_pa_kernel(
         V, S, G = nc.vector, nc.scalar, nc.gpsimd
         with tc.manual_schedule():
             token_statistics(0, 0)
+            deviation(0, 0)
             token_statistics(0, 1)
+            deviation(0, 1)
             gamma_beta_columns()
             spread_bias(0, 0)
             spread_bias(1, 0)
             spread_bias(0, 1)
             spread_bias(1, 1)
-            copy_bias(0, 0)
-            deviation(0)
-            inverse_deviation(0)
+            inverse_deviation(0, 0)
             normalise(0, 0, 0, V)
-            normalise(0, 1, 0, V)
-            regroup_w(0, 0, 0, 0, scalar_copy)
-            regroup_w(0, 0, 0, 1, vector_copy)
             normalise(0, 0, 1, V)
+            inverse_deviation(0, 1)
+            normalise(0, 1, 0, V)
             normalise(0, 1, 1, V)
-            regroup_w(0, 0, 1, 0, vector_copy)
-            regroup_w(0, 0, 1, 1, vector_copy)
+            copy_bias(0, 0)
+            regroup_w(0, 0, 0, 0, vector_copy)
+            regroup_w(0, 0, 0, 1, vector_copy)
+            quantise_w(0, 0, 1, 0)
             transpose_and_scale(0, 0)
             transpose_and_scale(0, 1)
+            regroup_w(0, 0, 1, 0, vector_copy)
+            regroup_w(0, 0, 1, 1, vector_copy)
             regroup_h(0, 0, vector_copy)
-            quantise_w(0, 0)
             regroup_h(0, 1, vector_copy)
+            quantise_w(0, 0, 1, 1)
             quantise_h(0)
+            copy_bias(1, 0)
             regroup_w(0, 1, 0, 0, scalar_copy)
             regroup_w(0, 1, 0, 1, scalar_copy)
             queries(0, 0, 0)
             queries(0, 1, 0)
-            regroup_w(0, 1, 1, 0, vector_copy)
+            regroup_w(0, 1, 1, 0, scalar_copy)
             regroup_w(0, 1, 1, 1, vector_copy)
-            copy_bias(1, 0)
+            quantise_w(0, 1, 1, 0)
             add_u(0, 0, 0, True)
             copy_keys(0, 1, 0, True)
-            quantise_w(0, 1)
+            quantise_w(0, 1, 1, 1)
             copy_keys(0, 0, 0, True)
         add_v(0, 1, 0, G, True)
         add_v(0, 0, 0, G, True)
         add_u(0, 1, 0, True)
         token_statistics(1, 0)
-        token_statistics(1, 1)
         deviation(1)
         inverse_deviation(1)
-        for g in range(PASSES):
-            normalise(1, 0, g, V)
-            normalise(1, 1, g, V)
+        normalise(1, 0, 0, V)
+        normalise(1, 0, 1, V)
         copy_bias(0, 1)
         copy_bias(1, 1)
         queries(0, 0, 1)
+        copy_keys(0, 0, 1, True)
+        add_u(0, 0, 1, True)
+        add_v(0, 0, 1, G, True)
         queries(0, 1, 1)
-        for jj in range(2):
-            copy_keys(0, jj, 1, True)
-            add_u(0, jj, 1, True)
-            add_v(0, jj, 1, G, True)
+        copy_keys(0, 1, 1, True)
+        add_u(0, 1, 1, True)
+        add_v(0, 1, 1, G, True)
         transpose_and_scale(1, 0)
         transpose_and_scale(1, 1)
         regroup_h(1, 0, vector_copy)
@@ -407,6 +417,24 @@ def tile_multiheadattentiowithrpe_pa_kernel(
         regroup_w(1, 0, 1, 0, scalar_copy)
         regroup_w(1, 0, 1, 1, scalar_copy)
         quantise_w(1, 0)
+        token_statistics(2, 0)
+        deviation(2)
+        inverse_deviation(2)
+        normalise(2, 0, 0, V)
+        normalise(2, 0, 1, V)
+        queries(1, 0, 0)
+        copy_keys(1, 0, 0)
+        add_u(1, 0, 0)
+        add_v(1, 0, 0, G)
+        queries(1, 0, 1)
+        copy_keys(1, 0, 1)
+        add_u(1, 0, 1)
+        add_v(1, 0, 1, G)
+        transpose_and_scale(2, 0)
+        transpose_and_scale(2, 1)
+        regroup_h(2, 0, vector_copy)
+        regroup_h(2, 1, vector_copy)
+        quantise_h(2)
         values(0, 0, 0, True)
         values(0, 1, 0, True)
         regroup_w(1, 1, 0, 0, vector_copy)
@@ -416,69 +444,95 @@ def tile_multiheadattentiowithrpe_pa_kernel(
         quantise_w(1, 1)
         values(0, 0, 1, True)
         values(0, 1, 1, True)
-        token_statistics(2, 0)
-        token_statistics(2, 1)
-        deviation(2)
-        inverse_deviation(2)
-        for g in range(PASSES):
-            normalise(2, 0, g, V)
-            normalise(2, 1, g, V)
-        for half in range(HALVES):
-            queries(1, 0, half)
-            copy_keys(1, 0, half)
-            add_u(1, 0, half)
-            add_v(1, 0, half, G)
-        for half in range(HALVES):
-            queries(1, 1, half)
-            copy_keys(1, 1, half)
-            add_u(1, 1, half)
-            add_v(1, 1, half, G)
-        transpose_and_scale(2, 0)
-        transpose_and_scale(2, 1)
-        regroup_h(2, 0, vector_copy)
-        regroup_h(2, 1, vector_copy)
-        quantise_h(2)
         values(1, 0, 0)
         values(1, 0, 1)
-        values(1, 1, 0)
-        values(1, 1, 1)
         token_statistics(3, 0)
-        token_statistics(3, 1)
         deviation(3)
         inverse_deviation(3)
-        for g in range(PASSES):
-            normalise(3, 0, g, V)
-            normalise(3, 1, g, V)
-        for half in range(HALVES):
-            queries(2, 0, half)
-            copy_keys(2, 0, half)
-            add_u(2, 0, half)
-            add_v(2, 0, half, G)
-        values(2, 0, 0)
-        values(2, 0, 1)
+        normalise(3, 0, 0, V)
+        normalise(3, 0, 1, V)
+        queries(2, 0, 0)
+        copy_keys(2, 0, 0)
+        add_u(2, 0, 0)
+        add_v(2, 0, 0, G)
+        queries(2, 0, 1)
+        copy_keys(2, 0, 1)
+        add_u(2, 0, 1)
+        add_v(2, 0, 1, G)
         transpose_and_scale(3, 0)
         transpose_and_scale(3, 1)
         regroup_h(3, 0, vector_copy)
         regroup_h(3, 1, vector_copy)
         quantise_h(3)
-        for half in range(HALVES):
-            queries(2, 1, half)
-            copy_keys(2, 1, half)
-            add_u(2, 1, half)
-            add_v(2, 1, half, G)
-        values(2, 1, 0)
-        values(2, 1, 1)
-        for half in range(HALVES):
-            queries(3, 0, half)
-            copy_keys(3, 0, half)
-            add_u(3, 0, half)
-            add_v(3, 0, half, G)
+        values(2, 0, 0)
+        values(2, 0, 1)
+        token_statistics(4, 0)
+        deviation(4)
+        inverse_deviation(4)
+        normalise(4, 0, 0, V)
+        normalise(4, 0, 1, V)
+        queries(3, 0, 0)
+        copy_keys(3, 0, 0)
+        add_u(3, 0, 0)
+        add_v(3, 0, 0, G)
+        queries(3, 0, 1)
+        copy_keys(3, 0, 1)
+        add_u(3, 0, 1)
+        add_v(3, 0, 1, G)
+        transpose_and_scale(4, 0)
+        transpose_and_scale(4, 1)
+        regroup_h(4, 0, vector_copy)
+        regroup_h(4, 1, vector_copy)
+        quantise_h(4)
         values(3, 0, 0)
         values(3, 0, 1)
-        for half in range(HALVES):
-            queries(3, 1, half)
-            copy_keys(3, 1, half)
-            add_u(3, 1, half)
-            add_v(3, 1, half, V)
-        values(3, 1, 0)
-        values(3, 1, 1)
+        token_statistics(5, 0)
+        deviation(5)
+        inverse_deviation(5)
+        normalise(5, 0, 0, V)
+        normalise(5, 0, 1, V)
+        queries(4, 0, 0)
+        copy_keys(4, 0, 0)
+        add_u(4, 0, 0)
+        add_v(4, 0, 0, G)
+        queries(4, 0, 1)
+        copy_keys(4, 0, 1)
+        add_u(4, 0, 1)
+        add_v(4, 0, 1, G)
+        transpose_and_scale(5, 0)
+        transpose_and_scale(5, 1)
+        regroup_h(5, 0, vector_copy)
+        regroup_h(5, 1, vector_copy)
+        quantise_h(5)
+        values(4, 0, 0)
+        values(4, 0, 1)
+        token_statistics(6, 0)
+        deviation(6)
+        inverse_deviation(6)
+        normalise(6, 0, 0, V)
+        normalise(6, 0, 1, V)
+        queries(5, 0, 0)
+        copy_keys(5, 0, 0)
+        add_u(5, 0, 0)
+        add_v(5, 0, 0, G)
+        queries(5, 0, 1)
+        copy_keys(5, 0, 1)
+        add_u(5, 0, 1)
+        add_v(5, 0, 1, G)
+        transpose_and_scale(6, 0)
+        transpose_and_scale(6, 1)
+        regroup_h(6, 0, vector_copy)
+        regroup_h(6, 1, vector_copy)
+        quantise_h(6)
+        values(5, 0, 0)
+        values(5, 0, 1)
+        queries(6, 0, 0)
+        copy_keys(6, 0, 0)
+        add_u(6, 0, 0)
+        add_v(6, 0, 0, V)
+        queries(6, 0, 1)
+        copy_keys(6, 0, 1)
+        add_u(6, 0, 1)
+        add_v(6, 0, 1, V)
+        values(6, 0, 0)
+        values(6, 0, 1)

@@ -27,6 +27,7 @@ HALVES = FEATURES // N_TILE
 W_PIECE = 256
 BN_WIDTH = 512
 EPS = 1e-5
+WARM = 3
 V_PIECE = 256
 
 FLOPS = 2 * TOKENS * D_MODEL * 2 * FEATURES
@@ -269,6 +270,12 @@ def tile_multiheadattentiowithrpe_pa_kernel(
             )
             copy(out=dst, in_=src)
 
+        def warm_tensor(grp):
+            scratch = psum_t.tile([P, N_TILE], F32, name="scratch", tag="xt")
+            flat = h_grouped[grp][:].rearrange("p g r t -> p (g r t)")
+            for n in range(WARM):
+                nc.tensor.matmul(scratch[:], lhsT=ident_bf[:], rhs=flat[:, 0:N_TILE], start=True, stop=True)
+
         def quantise_h(grp):
             nc.vector.quantize_mx(
                 out=h_codes[grp][:].bitcast(FP8X4),
@@ -332,10 +339,17 @@ def tile_multiheadattentiowithrpe_pa_kernel(
             j = GROUPS[grp][jj]
             if j not in with_v:
                 with_v[j] = stage.tile([P, FEATURES], F32, name="with_v", tag="with_v")
-            for c0 in range(half * N_TILE, (half + 1) * N_TILE, V_PIECE):
-                piece = slice(c0, c0 + V_PIECE)
-                src = keys[j][:, piece] if engine is nc.gpsimd else banks[(grp, jj, half)][:, c0 - half * N_TILE : c0 - half * N_TILE + V_PIECE]
-                engine.tensor_tensor(out=with_v[j][:, piece], in0=src, in1=bias_all[:, 1, piece], op=ALU.add)
+            cols = slice(half * N_TILE, (half + 1) * N_TILE)
+            if engine is nc.vector:
+                nc.vector.tensor_tensor(
+                    out=with_v[j][:, cols], in0=banks[(grp, jj, half)][:], in1=bias_all[:, 1, cols], op=ALU.add
+                )
+            else:
+                for c0 in range(half * N_TILE, (half + 1) * N_TILE, V_PIECE):
+                    piece = slice(c0, c0 + V_PIECE)
+                    nc.gpsimd.tensor_tensor(
+                        out=with_v[j][:, piece], in0=keys[j][:, piece], in1=bias_all[:, 1, piece], op=ALU.add
+                    )
             store(1, j, with_v[j], half, split)
 
         def values(grp, jj, half, split=False):
@@ -375,6 +389,7 @@ def tile_multiheadattentiowithrpe_pa_kernel(
             regroup_w(0, 0, 1, 1, vector_copy)
             regroup_h(0, 0, vector_copy)
             regroup_h(0, 1, vector_copy)
+            warm_tensor(0)
             quantise_w(0, 0, 1, 1)
             quantise_h(0)
             copy_bias(1, 0)
@@ -412,11 +427,6 @@ def tile_multiheadattentiowithrpe_pa_kernel(
         regroup_h(1, 0, vector_copy)
         regroup_h(1, 1, vector_copy)
         quantise_h(1)
-        regroup_w(1, 0, 0, 0, scalar_copy)
-        regroup_w(1, 0, 0, 1, scalar_copy)
-        regroup_w(1, 0, 1, 0, scalar_copy)
-        regroup_w(1, 0, 1, 1, scalar_copy)
-        quantise_w(1, 0)
         token_statistics(2, 0)
         deviation(2)
         inverse_deviation(2)
@@ -435,13 +445,28 @@ def tile_multiheadattentiowithrpe_pa_kernel(
         regroup_h(2, 0, vector_copy)
         regroup_h(2, 1, vector_copy)
         quantise_h(2)
+        regroup_w(1, 0, 0, 0, scalar_copy, W_PIECE // 2)
+        regroup_w(1, 0, 0, 1, scalar_copy, W_PIECE // 2)
+        regroup_w(1, 0, 0, 2, scalar_copy, W_PIECE // 2)
+        regroup_w(1, 0, 0, 3, scalar_copy, W_PIECE // 2)
+        quantise_w(1, 0, 1, 0)
+        regroup_w(1, 0, 1, 0, scalar_copy, W_PIECE // 2)
+        regroup_w(1, 0, 1, 1, scalar_copy, W_PIECE // 2)
+        regroup_w(1, 0, 1, 2, scalar_copy, W_PIECE // 2)
+        regroup_w(1, 0, 1, 3, scalar_copy, W_PIECE // 2)
+        quantise_w(1, 0, 1, 1)
         values(0, 0, 0, True)
         values(0, 1, 0, True)
-        regroup_w(1, 1, 0, 0, vector_copy)
-        regroup_w(1, 1, 0, 1, vector_copy)
-        regroup_w(1, 1, 1, 0, scalar_copy)
-        regroup_w(1, 1, 1, 1, scalar_copy)
-        quantise_w(1, 1)
+        regroup_w(1, 1, 0, 0, vector_copy, W_PIECE // 2)
+        regroup_w(1, 1, 0, 1, vector_copy, W_PIECE // 2)
+        regroup_w(1, 1, 0, 2, vector_copy, W_PIECE // 2)
+        regroup_w(1, 1, 0, 3, vector_copy, W_PIECE // 2)
+        quantise_w(1, 1, 1, 0)
+        regroup_w(1, 1, 1, 0, scalar_copy, W_PIECE // 2)
+        regroup_w(1, 1, 1, 1, scalar_copy, W_PIECE // 2)
+        regroup_w(1, 1, 1, 2, scalar_copy, W_PIECE // 2)
+        regroup_w(1, 1, 1, 3, scalar_copy, W_PIECE // 2)
+        quantise_w(1, 1, 1, 1)
         values(0, 0, 1, True)
         values(0, 1, 1, True)
         values(1, 0, 0)

@@ -21,7 +21,7 @@ PASSES = D_MODEL // K_PASS
 PLANES = PASSES * PACK
 TOKEN_TILES = TOKENS // P
 GROUPS = ((0, 1), (2,), (3,), (4,), (5,), (6,), (7,))
-EARLY_GROUPS = 3
+X_LOADS = ((0,), (1,), (2, 3), (4, 5, 6, 7))
 N_TILE = 512
 HALVES = FEATURES // N_TILE
 W_PIECE = 256
@@ -72,37 +72,32 @@ def tile_multiheadattentiowithrpe_pa_kernel(
         warm = const.tile([P, 1], F32, name="warm")
         nc.scalar.activation(out=warm[:], in_=eps[:], func=ACT.Sqrt)
 
-        x_sb = [
-            keep.tile([P, len(tiles), D_MODEL], BF16, name="x_sb%d" % grp) for grp, tiles in enumerate(GROUPS)
-        ]
+        x_tiles = [keep.tile([P, len(tiles), D_MODEL], BF16, name="x%d" % tiles[0]) for tiles in X_LOADS]
+        x_cols = {j: x_tiles[n][:, i, :] for n, tiles in enumerate(X_LOADS) for i, j in enumerate(tiles)}
         w_raw = [
             [keep.tile([P, PACK, FEATURES], BF16, name="w_raw%d%d" % (w, g)) for g in range(PASSES)] for w in range(2)
         ]
 
-        def load_x(grp):
-            tiles = GROUPS[grp]
-            nc.sync.dma_start(out=x_sb[grp][:], in_=x_view[:, tiles[0] : tiles[-1] + 1, :])
-
-        def load_x_tile(grp, jj):
-            nc.sync.dma_start(out=x_sb[grp][:, jj, :], in_=x_view[:, GROUPS[grp][jj], :])
+        def load_x(n):
+            tiles = X_LOADS[n]
+            nc.sync.dma_start(out=x_tiles[n][:], in_=x_view[:, tiles[0] : tiles[-1] + 1, :])
 
         def load_w(w):
             for g in range(PASSES):
                 nc.sync.dma_start(out=w_raw[w][g][:], in_=w_views[w][g])
 
-        load_x_tile(0, 0)
-        load_x_tile(0, 1)
+        load_x(0)
+        load_x(1)
         for i, vec in enumerate((u_bias.rearrange("h f -> (h f)"), v_bias.rearrange("h f -> (h f)"), gamma, beta)):
             nc.sync.dma_start(out=rows[2 * i : 2 * i + 2, :], in_=vec.rearrange("(r n) -> r n", n=N_TILE))
         load_w(0)
-        for grp in range(1, EARLY_GROUPS):
-            load_x(grp)
+        load_x(2)
         load_w(1)
-        for grp in range(EARLY_GROUPS, len(GROUPS)):
-            load_x(grp)
+        for n in range(3, len(X_LOADS)):
+            load_x(n)
 
         gb_cols = const.tile([P, 2 * PLANES], F32, name="gb_cols")
-        bias_all = const.tile([P, 2, FEATURES], F32, name="bias_all")
+        bias_all = const.tile([P, 2, FEATURES], BF16, name="bias_all")
 
         def gamma_beta_columns():
             cols_ps = psum_t.tile([P, PACK, 4], F32, name="cols_ps", tag="xt")
@@ -116,18 +111,20 @@ def tile_multiheadattentiowithrpe_pa_kernel(
 
         bias_ps = {}
 
-        def spread_bias(b, half):
-            bias_ps[(b, half)] = psum_o.tile([P, N_TILE], F32, name="bias_ps", tag="acc")
-            nc.tensor.matmul(
-                bias_ps[(b, half)][:],
-                lhsT=ident_bf[:, 2 * b + half : 2 * b + half + 1].to_broadcast([P, P]),
-                rhs=rows[:],
-                start=True,
-                stop=True,
-            )
+        def spread_bias(b):
+            bias_ps[b] = psum_o.tile([P, FEATURES], BF16, name="bias_ps", tag="acc")
+            for half in range(HALVES):
+                r = 2 * b + half
+                nc.tensor.matmul(
+                    bias_ps[b][:, half * N_TILE : (half + 1) * N_TILE],
+                    lhsT=ident_bf[:, r : r + 1].to_broadcast([P, P]),
+                    rhs=rows[:],
+                    start=True,
+                    stop=True,
+                )
 
-        def copy_bias(b, half):
-            nc.scalar.copy(out=bias_all[:, b, half * N_TILE : (half + 1) * N_TILE], in_=bias_ps[(b, half)][:])
+        def copy_bias(b):
+            nc.scalar.copy(out=bias_all[:, b, :], in_=bias_ps[b][:])
 
         h_codes = [
             keep.tile([P, PASSES * len(tiles) * P], U32, name="h_codes%d" % grp, align_bytes=64)
@@ -185,7 +182,7 @@ def tile_multiheadattentiowithrpe_pa_kernel(
             stats = small.tile([P, D_MODEL // BN_WIDTH, 6], F32, name="stats", tag="stats")
             for s in range(D_MODEL // BN_WIDTH):
                 nc.vector.bn_stats(
-                    out=stats[:, s, :], in_=x_sb[grp][:, jj, s * BN_WIDTH : (s + 1) * BN_WIDTH]
+                    out=stats[:, s, :], in_=x_cols[GROUPS[grp][jj]][:, s * BN_WIDTH : (s + 1) * BN_WIDTH]
                 )
             nc.vector.bn_aggr(out=mean_var[grp][:, jj, :], in_=stats[:].rearrange("p s v -> p (s v)"))
 
@@ -217,7 +214,7 @@ def tile_multiheadattentiowithrpe_pa_kernel(
                 normed[(grp, jj)] = work.tile([P, D_MODEL], F32, name="xn", tag="xn", bufs=4)
             cols = slice(g * K_PASS, (g + 1) * K_PASS)
             dst = normed[(grp, jj)][:, cols].rearrange("q (t p) -> q t p", t=PACK)
-            src = x_sb[grp][:, jj, cols].rearrange("q (p t) -> q t p", t=PACK)
+            src = x_cols[GROUPS[grp][jj]][:, cols].rearrange("q (p t) -> q t p", t=PACK)
             if engine is nc.scalar:
                 nc.scalar.activation(
                     out=dst,
@@ -369,17 +366,15 @@ def tile_multiheadattentiowithrpe_pa_kernel(
             token_statistics(0, 1)
             deviation(0, 1)
             gamma_beta_columns()
-            spread_bias(0, 0)
-            spread_bias(1, 0)
-            spread_bias(0, 1)
-            spread_bias(1, 1)
+            spread_bias(0)
+            spread_bias(1)
             inverse_deviation(0, 0)
             normalise(0, 0, 0, V)
             normalise(0, 0, 1, V)
             inverse_deviation(0, 1)
             normalise(0, 1, 0, V)
             normalise(0, 1, 1, V)
-            copy_bias(0, 0)
+            copy_bias(0)
             regroup_w(0, 0, 0, 0, vector_copy)
             regroup_w(0, 0, 0, 1, vector_copy)
             quantise_w(0, 0, 1, 0)
@@ -392,7 +387,7 @@ def tile_multiheadattentiowithrpe_pa_kernel(
             warm_tensor(0)
             quantise_w(0, 0, 1, 1)
             quantise_h(0)
-            copy_bias(1, 0)
+            copy_bias(1)
             regroup_w(0, 1, 0, 0, scalar_copy)
             regroup_w(0, 1, 0, 1, scalar_copy)
             queries(0, 0, 0)
@@ -412,8 +407,6 @@ def tile_multiheadattentiowithrpe_pa_kernel(
         inverse_deviation(1)
         normalise(1, 0, 0, V)
         normalise(1, 0, 1, V)
-        copy_bias(0, 1)
-        copy_bias(1, 1)
         queries(0, 0, 1)
         copy_keys(0, 0, 1, True)
         add_u(0, 0, 1, True)

from contextlib import ExitStack

import concourse.mybir as mybir
from concourse.masks import make_identity

F32 = mybir.dt.float32
BF16 = mybir.dt.bfloat16
U32 = mybir.dt.uint32
U8 = mybir.dt.uint8
FP8X4 = mybir.dt.float8_e4m3fn_x4
ACT = mybir.ActivationFunctionType
ALU = mybir.AluOpType

P = 128
PACK = 4
K_PASS = P * PACK
TOKENS = 1024
D_MODEL = 1024
FEATURES = 1024
PASSES = D_MODEL // K_PASS
PLANES = PASSES * PACK
TOKEN_TILES = TOKENS // P
GROUPS = ((0, 1), (2,), (3,), (4,), (5,), (6,), (7,))
X_LOADS = ((0,), (1,), (2, 3), (4, 5, 6, 7))
N_TILE = 512
HALVES = FEATURES // N_TILE
W_PIECE = 256
BN_WIDTH = 512
EPS = 1e-5
WARM = 3
V_PIECE = 256

FLOPS = 2 * TOKENS * D_MODEL * 2 * FEATURES


def regroup_views(grouped, planes):
    dst = grouped.rearrange("p (c i) t -> p c t i", i=4)
    src = planes.rearrange("p t (c i) -> p c t i", i=4)
    return dst, src


def tile_multiheadattentiowithrpe_pa_kernel(
    tc, x, gamma, beta, Wq, Wv, u_bias, v_bias, out_0, out_1, out_2, out_3
):
    nc = tc.nc

    x_view = x.rearrange("i b d -> (i b) d").rearrange("(p j) d -> p j d", j=TOKEN_TILES)
    out_views = [
        o.rearrange("i b h f -> (i b) (h f)").rearrange("(p j) n -> p j n", j=TOKEN_TILES)
        for o in (out_0, out_1, out_2, out_3)
    ]
    w_views = [w.rearrange("(g p t) n -> g p t n", t=PACK, p=P) for w in (Wq, Wv)]

    with ExitStack() as ctx:
        const = ctx.enter_context(tc.tile_pool(name="const", bufs=1))
        keep = ctx.enter_context(tc.tile_pool(name="keep", bufs=1))
        small = ctx.enter_context(tc.tile_pool(name="small", bufs=4))
        work = ctx.enter_context(tc.tile_pool(name="work", bufs=2))
        stage = ctx.enter_context(tc.tile_pool(name="stage", bufs=3))
        psum_t = ctx.enter_context(tc.psum_pool(name="psum_t", bufs=3))
        psum_o = ctx.enter_context(tc.psum_pool(name="psum_o", bufs=5))

        ident_bf = const.tile([P, P], BF16, name="ident_bf")
        make_identity(nc, ident_bf[:])
        ident = const.tile([P, P], F32, name="ident")
        make_identity(nc, ident[:])

        rows = const.tile([P, N_TILE], BF16, name="rows")
        nc.vector.memset(rows[:], 0.0)
        eps = const.tile([P, 1], F32, name="eps")
        nc.vector.memset(eps[:], EPS)
        warm = const.tile([P, 1], F32, name="warm")
        nc.scalar.activation(out=warm[:], in_=eps[:], func=ACT.Sqrt)

        x_tiles = [keep.tile([P, len(tiles), D_MODEL], BF16, name="x%d" % tiles[0]) for tiles in X_LOADS]
        x_cols = {j: x_tiles[n][:, i, :] for n, tiles in enumerate(X_LOADS) for i, j in enumerate(tiles)}
        w_raw = [
            [keep.tile([P, PACK, FEATURES], BF16, name="w_raw%d%d" % (w, g)) for g in range(PASSES)] for w in range(2)
        ]

        def load_x(n):
            tiles = X_LOADS[n]
            nc.sync.dma_start(out=x_tiles[n][:], in_=x_view[:, tiles[0] : tiles[-1] + 1, :])

        def load_w(w):
            for g in range(PASSES):
                nc.sync.dma_start(out=w_raw[w][g][:], in_=w_views[w][g])

        load_x(0)
        load_x(1)
        for i, vec in enumerate((u_bias.rearrange("h f -> (h f)"), v_bias.rearrange("h f -> (h f)"), gamma, beta)):
            nc.sync.dma_start(out=rows[2 * i : 2 * i + 2, :], in_=vec.rearrange("(r n) -> r n", n=N_TILE))
        load_w(0)
        load_x(2)
        load_w(1)
        for n in range(3, len(X_LOADS)):
            load_x(n)

        gb_cols = const.tile([P, 2 * PLANES], F32, name="gb_cols")
        bias_all = const.tile([P, 2, FEATURES], BF16, name="bias_all")

        def gamma_beta_columns():
            cols_ps = psum_t.tile([P, PACK, 4], F32, name="cols_ps", tag="xt")
            for t in range(PACK):
                nc.tensor.matmul(
                    cols_ps[:, t, :], lhsT=rows[:, t:N_TILE:PACK], rhs=ident_bf[:, 4:8], start=True, stop=True
                )
            nc.vector.tensor_copy(
                out=gb_cols[:].rearrange("p (r t) -> p r t", t=PACK), in_=cols_ps[:].rearrange("p t r -> p r t")
            )

        bias_ps = {}

        def spread_bias(b):
            bias_ps[b] = psum_o.tile([P, FEATURES], BF16, name="bias_ps", tag="acc")
            for half in range(HALVES):
                r = 2 * b + half
                nc.tensor.matmul(
                    bias_ps[b][:, half * N_TILE : (half + 1) * N_TILE],
                    lhsT=ident_bf[:, r : r + 1].to_broadcast([P, P]),
                    rhs=rows[:],
                    start=True,
                    stop=True,
                )

        def copy_bias(b):
            nc.scalar.copy(out=bias_all[:, b, :], in_=bias_ps[b][:])

        h_codes = [
            keep.tile([P, PASSES * len(tiles) * P], U32, name="h_codes%d" % grp, align_bytes=64)
            for grp, tiles in enumerate(GROUPS)
        ]
        h_scales = [
            keep.tile([P, PASSES * len(tiles) * P], U8, name="h_scales%d" % grp, align_bytes=64)
            for grp, tiles in enumerate(GROUPS)
        ]
        w_codes = [
            [keep.tile([P, PASSES * N_TILE], U32, name="w_codes%d%d" % (w, h), align_bytes=64) for h in range(HALVES)]
            for w in range(2)
        ]
        w_scales = [
            [keep.tile([P, PASSES * N_TILE], U8, name="w_scales%d%d" % (w, h), align_bytes=64) for h in range(HALVES)]
            for w in range(2)
        ]
        w_grouped = [
            [
                work.tile([P, PASSES, N_TILE, PACK], BF16, name="w_grouped%d%d" % (w, h), bufs=1, align_bytes=64)
                for h in range(HALVES)
            ]
            for w in range(2)
        ]

        def gpsimd_copy(out, in_):
            nc.gpsimd.tensor_scalar(out=out, in0=in_, scalar1=1.0, scalar2=0.0, op0=ALU.mult, op1=ALU.add)

        def regroup_w(w, half, g, piece, copy, width=W_PIECE):
            c0 = piece * width
            n0 = half * N_TILE + c0
            dst, src = regroup_views(w_grouped[w][half][:, g, c0 : c0 + width, :], w_raw[w][g][:, :, n0 : n0 + width])
            copy(out=dst, in_=src)

        def quantise_w(w, half, passes=PASSES, first=0):
            cols = slice(first * N_TILE, (first + passes) * N_TILE)
            nc.vector.quantize_mx(
                out=w_codes[w][half][:, cols].bitcast(FP8X4),
                scales=w_scales[w][half][:, cols],
                in_=w_grouped[w][half][:, first : first + passes, :, :].rearrange("p g n t -> p (g n t)"),
            )

        mean_var = {}
        rstd = {}
        shift = {}
        std = {}
        normed = {}
        h_planes = {}
        h_grouped = {}

        def token_statistics(grp, jj):
            n = len(GROUPS[grp])
            if jj == 0:
                mean_var[grp] = small.tile([P, n, 2], F32, name="mean_var", tag="mean_var")
            stats = small.tile([P, D_MODEL // BN_WIDTH, 6], F32, name="stats", tag="stats")
            for s in range(D_MODEL // BN_WIDTH):
                nc.vector.bn_stats(
                    out=stats[:, s, :], in_=x_cols[GROUPS[grp][jj]][:, s * BN_WIDTH : (s + 1) * BN_WIDTH]
                )
            nc.vector.bn_aggr(out=mean_var[grp][:, jj, :], in_=stats[:].rearrange("p s v -> p (s v)"))

        def deviation(grp, jj=None):
            n = len(GROUPS[grp])
            if grp not in std:
                std[grp] = small.tile([P, n], F32, name="std", tag="std")
            cols = slice(0, n) if jj is None else slice(jj, jj + 1)
            nc.scalar.activation(
                out=std[grp][:, cols], in_=mean_var[grp][:, cols, 1], func=ACT.Sqrt, bias=eps[:, 0:1]
            )

        def inverse_deviation(grp, jj=None):
            n = len(GROUPS[grp])
            if grp not in rstd:
                rstd[grp] = small.tile([P, n], F32, name="rstd", tag="rstd")
            cols = slice(0, n) if jj is None else slice(jj, jj + 1)
            nc.vector.reciprocal(out=rstd[grp][:, cols], in_=std[grp][:, cols])

        def minus_mean(grp):
            n = len(GROUPS[grp])
            shift[grp] = small.tile([P, n], F32, name="shift", tag="shift")
            nc.vector.scalar_tensor_tensor(
                out=shift[grp][:], in0=mean_var[grp][:, :, 0], scalar=-1.0, in1=rstd[grp][:], op0=ALU.mult, op1=ALU.mult
            )

        def normalise(grp, jj, g, engine):
            if g == 0:
                normed[(grp, jj)] = work.tile([P, D_MODEL], F32, name="xn", tag="xn", bufs=4)
            cols = slice(g * K_PASS, (g + 1) * K_PASS)
            dst = normed[(grp, jj)][:, cols].rearrange("q (t p) -> q t p", t=PACK)
            src = x_cols[GROUPS[grp][jj]][:, cols].rearrange("q (p t) -> q t p", t=PACK)
            if engine is nc.scalar:
                nc.scalar.activation(
                    out=dst,
                    in_=src,
                    func=ACT.Identity,
                    scale=rstd[grp][:, jj : jj + 1],
                    bias=shift[grp][:, jj : jj + 1],
                )
            else:
                engine.tensor_scalar(
                    out=dst,
                    in0=src,
                    scalar1=mean_var[grp][:, jj, 0:1],
                    scalar2=rstd[grp][:, jj : jj + 1],
                    op0=ALU.subtract,
                    op1=ALU.mult,
                )

        def transpose_and_scale(grp, g):
            n = len(GROUPS[grp])
            per_bank = PACK // n
            if g == 0:
                h_planes[grp] = work.tile([P, PLANES, n * P], BF16, name="h_planes", tag="h_planes%d" % n)
            for c0 in range(g * PACK, (g + 1) * PACK, per_bank):
                xt = psum_t.tile([P, per_bank, n * P], F32, name="xt", tag="xt")
                for cc in range(per_bank):
                    c = c0 + cc
                    for jj in range(n):
                        nc.tensor.transpose(
                            xt[:, cc, jj * P : (jj + 1) * P], normed[(grp, jj)][:, c * P : (c + 1) * P], ident[:]
                        )
                for cc in range(per_bank):
                    c = c0 + cc
                    nc.scalar.activation(
                        out=h_planes[grp][:, c, :],
                        in_=xt[:, cc, :],
                        func=ACT.Identity,
                        scale=gb_cols[:, c : c + 1],
                        bias=gb_cols[:, PLANES + c : PLANES + c + 1],
                    )

        def regroup_h(grp, g, copy):
            n = len(GROUPS[grp])
            if g == 0:
                h_grouped[grp] = work.tile(
                    [P, PASSES, n * P, PACK], BF16, name="h_grouped", tag="h_grouped%d" % n, align_bytes=64
                )
            dst, src = regroup_views(
                h_grouped[grp][:, g, :, :], h_planes[grp][:, g * PACK : (g + 1) * PACK, :]
            )
            copy(out=dst, in_=src)

        def warm_tensor(grp):
            scratch = psum_t.tile([P, N_TILE], F32, name="scratch", tag="xt")
            flat = h_grouped[grp][:].rearrange("p g r t -> p (g r t)")
            for n in range(WARM):
                nc.tensor.matmul(scratch[:], lhsT=ident_bf[:], rhs=flat[:, 0:N_TILE], start=True, stop=True)

        def quantise_h(grp):
            nc.vector.quantize_mx(
                out=h_codes[grp][:].bitcast(FP8X4),
                scales=h_scales[grp][:],
                in_=h_grouped[grp][:].rearrange("p g r t -> p (g r t)"),
            )

        def project(grp, jj, w, half):
            n = len(GROUPS[grp])
            acc = psum_o.tile([P, N_TILE], F32, name="acc", tag="acc")
            for g in range(PASSES):
                h_cols = slice((g * n + jj) * P, (g * n + jj + 1) * P)
                w_cols = slice(g * N_TILE, (g + 1) * N_TILE)
                nc.tensor.matmul_mx(
                    out=acc[:],
                    lhsT=h_codes[grp][:, h_cols].bitcast(FP8X4),
                    lhsT_scale=h_scales[grp][:, h_cols],
                    rhs=w_codes[w][half][:, w_cols].bitcast(FP8X4),
                    rhs_scale=w_scales[w][half][:, w_cols],
                    start=(g == 0),
                    stop=(g == PASSES - 1),
                )
            return acc

        keys = {}
        halves_done = set()
        with_u = {}
        with_v = {}
        vals = {}
        banks = {}

        def queries(grp, jj, half):
            banks[(grp, jj, half)] = project(grp, jj, 0, half)

        def store(o, j, tile, half, split):
            if split:
                cols = slice(half * N_TILE, (half + 1) * N_TILE)
                nc.sync.dma_start(out=out_views[o][:, j, cols], in_=tile[:, cols])
            elif (o, j) in halves_done:
                nc.sync.dma_start(out=out_views[o][:, j, :], in_=tile[:])
            halves_done.add((o, j))

        def copy_keys(grp, jj, half, split=False):
            j = GROUPS[grp][jj]
            if j not in keys:
                keys[j] = stage.tile([P, FEATURES], F32, name="keys", tag="keys")
            nc.scalar.copy(out=keys[j][:, half * N_TILE : (half + 1) * N_TILE], in_=banks[(grp, jj, half)][:])
            store(2, j, keys[j], half, split)

        def add_u(grp, jj, half, split=False):
            j = GROUPS[grp][jj]
            if j not in with_u:
                with_u[j] = stage.tile([P, FEATURES], F32, name="with_u", tag="with_u")
            cols = slice(half * N_TILE, (half + 1) * N_TILE)
            nc.vector.tensor_tensor(
                out=with_u[j][:, cols], in0=banks[(grp, jj, half)][:], in1=bias_all[:, 0, cols], op=ALU.add
            )
            store(0, j, with_u[j], half, split)

        def add_v(grp, jj, half, engine, split=False):
            j = GROUPS[grp][jj]
            if j not in with_v:
                with_v[j] = stage.tile([P, FEATURES], F32, name="with_v", tag="with_v")
            cols = slice(half * N_TILE, (half + 1) * N_TILE)
            if engine is nc.vector:
                nc.vector.tensor_tensor(
                    out=with_v[j][:, cols], in0=banks[(grp, jj, half)][:], in1=bias_all[:, 1, cols], op=ALU.add
                )
            else:
                for c0 in range(half * N_TILE, (half + 1) * N_TILE, V_PIECE):
                    piece = slice(c0, c0 + V_PIECE)
                    nc.gpsimd.tensor_tensor(
                        out=with_v[j][:, piece], in0=keys[j][:, piece], in1=bias_all[:, 1, piece], op=ALU.add
                    )
            store(1, j, with_v[j], half, split)

        def values(grp, jj, half, split=False):
            j = GROUPS[grp][jj]
            if j not in vals:
                vals[j] = stage.tile([P, FEATURES], F32, name="vals", tag="vals")
            acc = project(grp, jj, 1, half)
            nc.scalar.copy(out=vals[j][:, half * N_TILE : (half + 1) * N_TILE], in_=acc[:])
            store(3, j, vals[j], half, split)

        vector_copy = nc.vector.tensor_copy
        scalar_copy = nc.scalar.copy
        V, S, G = nc.vector, nc.scalar, nc.gpsimd
        with tc.manual_schedule():
            token_statistics(0, 0)
            deviation(0, 0)
            token_statistics(0, 1)
            deviation(0, 1)
            gamma_beta_columns()
            spread_bias(0)
            spread_bias(1)
            inverse_deviation(0, 0)
            normalise(0, 0, 0, V)
            normalise(0, 0, 1, V)
            inverse_deviation(0, 1)
            normalise(0, 1, 0, V)
            normalise(0, 1, 1, V)
            copy_bias(0)
            regroup_w(0, 0, 0, 0, vector_copy)
            regroup_w(0, 0, 0, 1, vector_copy)
            quantise_w(0, 0, 1, 0)
            transpose_and_scale(0, 0)
            transpose_and_scale(0, 1)
            regroup_w(0, 0, 1, 0, vector_copy)
            regroup_w(0, 0, 1, 1, vector_copy)
            regroup_h(0, 0, vector_copy)
            regroup_h(0, 1, vector_copy)
            warm_tensor(0)
            quantise_w(0, 0, 1, 1)
            quantise_h(0)
            copy_bias(1)
            regroup_w(0, 1, 0, 0, scalar_copy)
            regroup_w(0, 1, 0, 1, scalar_copy)
            queries(0, 0, 0)
            queries(0, 1, 0)
            regroup_w(0, 1, 1, 0, scalar_copy)
            regroup_w(0, 1, 1, 1, vector_copy)
            quantise_w(0, 1, 1, 0)
            add_u(0, 0, 0, True)
            copy_keys(0, 1, 0, True)
            quantise_w(0, 1, 1, 1)
            copy_keys(0, 0, 0, True)
        add_v(0, 1, 0, G, True)
        add_v(0, 0, 0, G, True)
        add_u(0, 1, 0, True)
        token_statistics(1, 0)
        deviation(1)
        inverse_deviation(1)
        normalise(1, 0, 0, V)
        normalise(1, 0, 1, V)
        queries(0, 0, 1)
        copy_keys(0, 0, 1, True)
        add_u(0, 0, 1, True)
        add_v(0, 0, 1, G, True)
        queries(0, 1, 1)
        copy_keys(0, 1, 1, True)
        add_u(0, 1, 1, True)
        add_v(0, 1, 1, G, True)
        transpose_and_scale(1, 0)
        transpose_and_scale(1, 1)
        regroup_h(1, 0, vector_copy)
        regroup_h(1, 1, vector_copy)
        quantise_h(1)
        token_statistics(2, 0)
        deviation(2)
        inverse_deviation(2)
        normalise(2, 0, 0, V)
        normalise(2, 0, 1, V)
        queries(1, 0, 0)
        copy_keys(1, 0, 0)
        add_u(1, 0, 0)
        add_v(1, 0, 0, G)
        queries(1, 0, 1)
        copy_keys(1, 0, 1)
        add_u(1, 0, 1)
        add_v(1, 0, 1, G)
        transpose_and_scale(2, 0)
        transpose_and_scale(2, 1)
        regroup_h(2, 0, vector_copy)
        regroup_h(2, 1, vector_copy)
        quantise_h(2)
        regroup_w(1, 0, 0, 0, scalar_copy, W_PIECE // 2)
        regroup_w(1, 0, 0, 1, scalar_copy, W_PIECE // 2)
        regroup_w(1, 0, 0, 2, scalar_copy, W_PIECE // 2)
        regroup_w(1, 0, 0, 3, scalar_copy, W_PIECE // 2)
        quantise_w(1, 0, 1, 0)
        regroup_w(1, 0, 1, 0, scalar_copy, W_PIECE // 2)
        regroup_w(1, 0, 1, 1, scalar_copy, W_PIECE // 2)
        regroup_w(1, 0, 1, 2, scalar_copy, W_PIECE // 2)
        regroup_w(1, 0, 1, 3, scalar_copy, W_PIECE // 2)
        quantise_w(1, 0, 1, 1)
        values(0, 0, 0, True)
        values(0, 1, 0, True)
        regroup_w(1, 1, 0, 0, vector_copy, W_PIECE // 2)
        regroup_w(1, 1, 0, 1, vector_copy, W_PIECE // 2)
        regroup_w(1, 1, 0, 2, vector_copy, W_PIECE // 2)
        regroup_w(1, 1, 0, 3, vector_copy, W_PIECE // 2)
        quantise_w(1, 1, 1, 0)
        regroup_w(1, 1, 1, 0, scalar_copy, W_PIECE // 2)
        regroup_w(1, 1, 1, 1, scalar_copy, W_PIECE // 2)
        regroup_w(1, 1, 1, 2, scalar_copy, W_PIECE // 2)
        regroup_w(1, 1, 1, 3, scalar_copy, W_PIECE // 2)
        quantise_w(1, 1, 1, 1)
        values(0, 0, 1, True)
        values(0, 1, 1, True)
        values(1, 0, 0)
        values(1, 0, 1)
        token_statistics(3, 0)
        deviation(3)
        inverse_deviation(3)
        normalise(3, 0, 0, V)
        normalise(3, 0, 1, V)
        queries(2, 0, 0)
        copy_keys(2, 0, 0)
        add_u(2, 0, 0)
        add_v(2, 0, 0, G)
        queries(2, 0, 1)
        copy_keys(2, 0, 1)
        add_u(2, 0, 1)
        add_v(2, 0, 1, G)
        transpose_and_scale(3, 0)
        transpose_and_scale(3, 1)
        regroup_h(3, 0, vector_copy)
        regroup_h(3, 1, vector_copy)
        quantise_h(3)
        values(2, 0, 0)
        values(2, 0, 1)
        token_statistics(4, 0)
        deviation(4)
        inverse_deviation(4)
        normalise(4, 0, 0, V)
        normalise(4, 0, 1, V)
        queries(3, 0, 0)
        copy_keys(3, 0, 0)
        add_u(3, 0, 0)
        add_v(3, 0, 0, G)
        queries(3, 0, 1)
        copy_keys(3, 0, 1)
        add_u(3, 0, 1)
        add_v(3, 0, 1, G)
        transpose_and_scale(4, 0)
        transpose_and_scale(4, 1)
        regroup_h(4, 0, vector_copy)
        regroup_h(4, 1, vector_copy)
        quantise_h(4)
        values(3, 0, 0)
        values(3, 0, 1)
        token_statistics(5, 0)
        deviation(5)
        inverse_deviation(5)
        normalise(5, 0, 0, V)
        normalise(5, 0, 1, V)
        queries(4, 0, 0)
        copy_keys(4, 0, 0)
        add_u(4, 0, 0)
        add_v(4, 0, 0, G)
        queries(4, 0, 1)
        copy_keys(4, 0, 1)
        add_u(4, 0, 1)
        add_v(4, 0, 1, G)
        transpose_and_scale(5, 0)
        transpose_and_scale(5, 1)
        regroup_h(5, 0, vector_copy)
        regroup_h(5, 1, vector_copy)
        quantise_h(5)
        values(4, 0, 0)
        values(4, 0, 1)
        token_statistics(6, 0)
        deviation(6)
        inverse_deviation(6)
        normalise(6, 0, 0, V)
        normalise(6, 0, 1, V)
        queries(5, 0, 0)
        copy_keys(5, 0, 0)
        add_u(5, 0, 0)
        add_v(5, 0, 0, G)
        queries(5, 0, 1)
        copy_keys(5, 0, 1)
        add_u(5, 0, 1)
        add_v(5, 0, 1, G)
        transpose_and_scale(6, 0)
        transpose_and_scale(6, 1)
        regroup_h(6, 0, vector_copy)
        regroup_h(6, 1, vector_copy)
        quantise_h(6)
        values(5, 0, 0)
        values(5, 0, 1)
        queries(6, 0, 0)
        copy_keys(6, 0, 0)
        add_u(6, 0, 0)
        add_v(6, 0, 0, V)
        queries(6, 0, 1)
        copy_keys(6, 0, 1)
        add_u(6, 0, 1)
        add_v(6, 0, 1, V)
        values(6, 0, 0)
        values(6, 0, 1)
